import numpy as np
import ml_dtypes


def mxq(x, axis, fmt="e4m3"):
    dtype, down = {"e4m3": (ml_dtypes.float8_e4m3fn, 7), "e5m2": (ml_dtypes.float8_e5m2, 14)}[fmt]
    v = np.moveaxis(np.asarray(x, np.float32).astype(ml_dtypes.bfloat16).astype(np.float64), axis, -1)
    blocks = v.reshape(v.shape[:-1] + (-1, 32))
    amax = np.abs(blocks).max(-1, keepdims=True)
    byte = np.maximum(np.where(amax > 0, np.frexp(amax)[1] - 1 + 127, 0) - down, 1)
    scale = np.exp2(byte - 127.0)
    codes = (blocks / scale).astype(np.float32).astype(dtype).astype(np.float64)
    return np.moveaxis((codes * scale).reshape(v.shape), -1, axis)


WIDE = False


def mx_kscale(k):
    if not WIDE:
        return np.ones(k)
    levels = np.array([10, -10, 5, -5, 0])
    if k % 512:
        return np.exp2(np.random.permutation(np.resize(levels, k // 32))).repeat(32)
    a = np.empty((k // 512, 16))
    for p in range(k // 512):
        a[p, :8] = np.random.permutation(np.resize(levels, 8))
        for g in range(8):
            far = levels[np.abs(levels - a[p, g]) >= 10]
            a[p, g + 8] = far[np.random.randint(len(far))]
    return np.exp2(a.ravel()).repeat(32)


BF16 = ml_dtypes.bfloat16


def bf(x):
    return np.asarray(x, np.float32).astype(BF16)


def f64(x):
    return np.asarray(x).astype(np.float64)


T, B, D, U, V, E = 4, 8192, 1024, 16, 512, 8
G = 2 * E
GS = (T + 1) * E


def softmax(v):
    e = np.exp(v - v.max(-1, keepdims=True))
    return e / e.sum(-1, keepdims=True)


def setup_inputs():
    rn = np.random.standard_normal
    s = mx_kscale(D)
    return {
        "x": bf(rn((B, D)) * s),
        "ews0": bf(rn((D, U, E)) / np.sqrt(D) / s[:, None, None]),
        "ebs0": bf(rn((U, E)) * 0.5),
        "ew0": bf(rn((T, D, U, E)) / np.sqrt(D) / s[None, :, None, None]),
        "eb0": bf(rn((T, U, E)) * 0.5),
        "gate_pre0": bf(rn((T, B, G))),
        "gb0": bf(rn((T, G)) * 0.5),
        "sgate_pre": bf(rn((B, GS))),
        "gbs": bf(rn((GS,)) * 0.5),
    }


def reference(x, ews0, ebs0, ew0, eb0, gate_pre0, gb0, sgate_pre, gbs):
    xq = mxq(f64(x), 1, "e4m3")
    es = np.maximum((xq @ mxq(f64(ews0).reshape(D, U * E), 0, "e4m3")).reshape(B, U, E) + f64(ebs0), 0.0)
    et = np.maximum((xq @ mxq(f64(ew0).reshape(T, D, U * E), 1, "e4m3")).reshape(T, B, U, E) + f64(eb0)[:, None], 0.0)
    g = softmax(f64(gate_pre0) + f64(gb0)[:, None])
    comb = np.concatenate([et, np.broadcast_to(es, et.shape)], axis=-1)
    task_out = (comb * g[:, :, None, :]).sum(-1)
    gs = softmax(f64(sgate_pre) + f64(gbs))
    all_exp = np.concatenate([np.moveaxis(et, 0, 2).reshape(B, U, T * E), es], axis=-1)
    share_out = (all_exp * gs[:, None, :]).sum(-1)
    return task_out, share_out

@@ -1,0 +1,469 @@
+from contextlib import ExitStack
+
+import concourse.mybir as mybir
+from concourse.masks import make_identity
+
+F32 = mybir.dt.float32
+BF16 = mybir.dt.bfloat16
+U32 = mybir.dt.uint32
+U8 = mybir.dt.uint8
+FP8X4 = mybir.dt.float8_e4m3fn_x4
+ALU = mybir.AluOpType
+ACT = mybir.ActivationFunctionType
+AXIS_X = mybir.AxisListType.X
+
+P = 128
+T, B, D, U, E = 4, 8192, 1024, 16, 8
+SOURCES = T + 1
+SHARED = T
+UE = U * E
+G_TASK = 2 * E
+G_SHARE = SOURCES * E
+PACK = 4
+K_PASS = P * PACK
+PASSES = D // K_PASS
+ROW_TILES = B // P
+ROUND = 4
+ROUNDS = ROW_TILES // ROUND
+COLS = ROUND * P
+GATE_CHUNK = 16
+STORE_ROUNDS = 4
+SLOTS_USED = SOURCES * U
+
+FLOPS = 2 * B * D * SOURCES * UE
+
+
+def tile_plelayer_pa_t_kernel(
+    tc, x, ews0, ebs0, ew0, eb0, gate_pre0, gb0, sgate_pre, gbs, out_0, out_1
+):
+    nc = tc.nc
+    with ExitStack() as ctx:
+        keep = ctx.enter_context(tc.tile_pool(name="keep", bufs=1))
+        gate_tmp = ctx.enter_context(tc.tile_pool(name="gate_tmp", bufs=2))
+        x_pool = ctx.enter_context(tc.tile_pool(name="x_pool", bufs=3))
+        work = ctx.enter_context(tc.tile_pool(name="work", bufs=2))
+        prod = ctx.enter_context(tc.tile_pool(name="prod", bufs=2 * ROUND))
+        ps_xt = ctx.enter_context(tc.psum_pool(name="ps_xt", bufs=2))
+        ps_y = ctx.enter_context(tc.psum_pool(name="ps_y", bufs=2))
+        ps_own = ctx.enter_context(tc.psum_pool(name="ps_own", bufs=2))
+        ps_misc = ctx.enter_context(tc.psum_pool(name="ps_misc", bufs=2))
+        ctx.enter_context(tc.manual_schedule())
+
+        x_rows = x.rearrange("(p n) k -> p n k", n=ROW_TILES)
+        out_task_rows = out_0.rearrange("t (p n) u -> p t n u", n=ROW_TILES)
+        out_share_rows = out_1.rearrange("(p n) u -> p n u", n=ROW_TILES)
+
+        SHARED_ROW = 32
+        bias_rows = keep.tile([P, UE], BF16)
+        nc.scalar.dma_start(out=bias_rows[0:T, :], in_=eb0.rearrange("t u e -> t (u e)"))
+        nc.scalar.dma_start(
+            out=bias_rows[SHARED_ROW : SHARED_ROW + 1, :],
+            in_=ebs0.rearrange("(o u) e -> o (u e)", o=1),
+        )
+        gate_bias_task = keep.tile([P, T, G_TASK], BF16)
+        nc.scalar.dma_start(
+            out=gate_bias_task[:].rearrange("p t k -> p (t k)"),
+            in_=gb0.rearrange("t k -> (t k)").partition_broadcast(P),
+        )
+        gate_bias_share = keep.tile([P, G_SHARE], BF16)
+        nc.scalar.dma_start(out=gate_bias_share[:], in_=gbs.partition_broadcast(P))
+        pre_task = keep.tile([P, T, ROW_TILES, G_TASK], BF16)
+        pre_share = keep.tile([P, ROW_TILES, G_SHARE], BF16)
+        pre_task_rows = gate_pre0.rearrange("t (p n) k -> p t n k", n=ROW_TILES)
+        pre_share_rows = sgate_pre.rearrange("(p n) k -> p n k", n=ROW_TILES)
+        nc.scalar.dma_start(out=pre_task[:, :, 0:ROUND, :], in_=pre_task_rows[:, :, 0:ROUND, :])
+        nc.scalar.dma_start(out=pre_share[:, 0:ROUND, :], in_=pre_share_rows[:, 0:ROUND, :])
+        w_raw = keep.tile([P, SOURCES, PASSES, PACK, UE], BF16)
+        for t in range(T):
+            nc.sync.dma_start(
+                out=w_raw[:, t],
+                in_=ew0[t].rearrange("(g q j) u e -> q g j (u e)", g=PASSES, j=PACK),
+            )
+        nc.sync.dma_start(
+            out=w_raw[:, SHARED],
+            in_=ews0.rearrange("(g q j) u e -> q g j (u e)", g=PASSES, j=PACK),
+        )
+
+        x_tiles = {}
+
+        def load_x(r):
+            x_sb = x_pool.tile([P, ROUND, D], BF16)
+            nc.sync.dma_start(out=x_sb[:], in_=x_rows[:, r * ROUND : (r + 1) * ROUND, :])
+            x_tiles[r] = x_sb
+
+        X_AHEAD = 3
+        load_x(0)
+        nc.sync.dma_start(
+            out=pre_task[:, :, ROUND:ROW_TILES, :], in_=pre_task_rows[:, :, ROUND:ROW_TILES, :]
+        )
+        nc.sync.dma_start(
+            out=pre_share[:, ROUND:ROW_TILES, :], in_=pre_share_rows[:, ROUND:ROW_TILES, :]
+        )
+        for r in range(1, X_AHEAD):
+            load_x(r)
+
+        ident = keep.tile([P, P], F32)
+        make_identity(nc, ident[:])
+
+        gates_own = keep.tile([P, ROW_TILES, E, 2, T], F32)
+        gates_shared = keep.tile([P, ROW_TILES, SOURCES, E], F32)
+
+        def gate_job(first_row_tile, count):
+            task_tile = gate_tmp.tile([P, T, GATE_CHUNK, G_TASK], F32)
+            share_tile = gate_tmp.tile([P, GATE_CHUNK, G_SHARE], F32)
+            task_top = gate_tmp.tile([P, T, GATE_CHUNK], F32)
+            share_top = gate_tmp.tile([P, GATE_CHUNK], F32)
+            task_sum = gate_tmp.tile([P, T, GATE_CHUNK], F32)
+            share_sum = gate_tmp.tile([P, GATE_CHUNK], F32)
+            task_inv = gate_tmp.tile([P, T, GATE_CHUNK], F32)
+            share_inv = gate_tmp.tile([P, GATE_CHUNK], F32)
+            return {
+                "rows": slice(first_row_tile, first_row_tile + count),
+                "count": count,
+                "task": task_tile[:, :, 0:count, :],
+                "share": share_tile[:, 0:count, :],
+                "task_top": task_top[:, :, 0:count],
+                "share_top": share_top[:, 0:count],
+                "task_sum": task_sum[:, :, 0:count],
+                "share_sum": share_sum[:, 0:count],
+                "task_inv": task_inv[:, :, 0:count],
+                "share_inv": share_inv[:, 0:count],
+            }
+
+        def gates_logits(job):
+            rows, count = job["rows"], job["count"]
+            nc.gpsimd.tensor_tensor(
+                out=job["task"],
+                in0=pre_task[:, :, rows, :],
+                in1=gate_bias_task[:].unsqueeze(2).to_broadcast([P, T, count, G_TASK]),
+                op=ALU.add,
+            )
+            nc.gpsimd.tensor_tensor(
+                out=job["share"],
+                in0=pre_share[:, rows, :],
+                in1=gate_bias_share[:].unsqueeze(1).to_broadcast([P, count, G_SHARE]),
+                op=ALU.add,
+            )
+
+        def gates_top(job):
+            nc.vector.tensor_reduce(out=job["task_top"], in_=job["task"], axis=AXIS_X, op=ALU.max)
+            nc.vector.tensor_reduce(out=job["share_top"], in_=job["share"], axis=AXIS_X, op=ALU.max)
+
+        def gates_subtract(job):
+            count = job["count"]
+            nc.gpsimd.tensor_tensor(
+                out=job["task"],
+                in0=job["task"],
+                in1=job["task_top"].unsqueeze(3).to_broadcast([P, T, count, G_TASK]),
+                op=ALU.subtract,
+            )
+            nc.gpsimd.tensor_tensor(
+                out=job["share"],
+                in0=job["share"],
+                in1=job["share_top"].unsqueeze(2).to_broadcast([P, count, G_SHARE]),
+                op=ALU.subtract,
+            )
+
+        def gates_exp(job):
+            nc.scalar.activation(out=job["task"], in_=job["task"], func=ACT.Exp)
+            nc.scalar.activation(out=job["share"], in_=job["share"], func=ACT.Exp)
+
+        def gates_inverse(job):
+            nc.vector.tensor_reduce(out=job["task_sum"], in_=job["task"], axis=AXIS_X, op=ALU.add)
+            nc.vector.tensor_reduce(out=job["share_sum"], in_=job["share"], axis=AXIS_X, op=ALU.add)
+            nc.vector.reciprocal(out=job["task_inv"], in_=job["task_sum"])
+            nc.vector.reciprocal(out=job["share_inv"], in_=job["share_sum"])
+
+        def gates_write(job):
+            rows, count = job["rows"], job["count"]
+            task_inv_nt = job["task_inv"].rearrange("p t n -> p n t")
+            nc.gpsimd.tensor_tensor(
+                out=gates_shared[:, rows, 0:T, :],
+                in0=job["task"][:, :, :, E:G_TASK].rearrange("p t n e -> p n t e"),
+                in1=task_inv_nt.unsqueeze(3).to_broadcast([P, count, T, E]),
+                op=ALU.mult,
+            )
+            nc.gpsimd.tensor_tensor(
+                out=gates_shared[:, rows, SHARED, :],
+                in0=job["share"][:, :, T * E : G_SHARE],
+                in1=job["share_inv"].unsqueeze(2).to_broadcast([P, count, E]),
+                op=ALU.mult,
+            )
+            nc.gpsimd.tensor_tensor(
+                out=gates_own[:, rows, :, 0, :],
+                in0=job["task"][:, :, :, 0:E].rearrange("p t n e -> p n e t"),
+                in1=task_inv_nt.unsqueeze(2).to_broadcast([P, count, E, T]),
+                op=ALU.mult,
+            )
+            nc.gpsimd.tensor_tensor(
+                out=gates_own[:, rows, :, 1, :],
+                in0=job["share"][:, :, 0 : T * E].rearrange("p n (t e) -> p n e t", t=T),
+                in1=job["share_inv"].unsqueeze(2).unsqueeze(3).to_broadcast([P, count, E, T]),
+                op=ALU.mult,
+            )
+
+        GATE_LEAD = 3
+        gate_job_rows = {1 - GATE_LEAD: (ROUND, GATE_CHUNK - ROUND)}
+        for chunk in range(1, ROW_TILES // GATE_CHUNK):
+            gate_job_rows[chunk * GATE_CHUNK // ROUND - GATE_LEAD] = (chunk * GATE_CHUNK, GATE_CHUNK)
+        gate_jobs = {}
+        first_job = gate_job(0, ROUND)
+
+        shared_sum_a = keep.tile([P, ROUND, P], F32)
+        shared_sum_b = keep.tile([P, ROUND, P], F32)
+        shared_sums = [shared_sum_a, shared_sum_b]
+        bias_square = keep.tile([P, P], F32)
+        nc.vector.memset(bias_square[:], 0.0)
+        for shared_sum in shared_sums:
+            nc.vector.memset(shared_sum[:], 0.0)
+
+        nc.vector.tensor_copy(
+            out=bias_square[0:T, :].rearrange("t (e u) -> t e u", e=E),
+            in_=bias_rows[0:T, :].rearrange("t (u e) -> t e u", e=E),
+        )
+        nc.vector.tensor_copy(
+            out=bias_square[SHARED_ROW : SHARED_ROW + 1, :],
+            in_=bias_rows[SHARED_ROW : SHARED_ROW + 1, :],
+        )
+        bias_ps = ps_misc.tile([P, P], F32, tag="misc")
+        nc.tensor.transpose(out=bias_ps[:], in_=bias_square[:], identity=ident[:])
+
+        gates_logits(first_job)
+        gates_top(first_job)
+        gates_subtract(first_job)
+
+        w_grouped = keep.tile([P, PASSES, SOURCES, UE, PACK], BF16, align_bytes=64)
+        w_codes = keep.tile([P, PASSES, SOURCES * UE], U32, align_bytes=64)
+        w_scales = keep.tile([P, PASSES, SOURCES * UE], U8, align_bytes=64)
+        VECTOR_GROUPS = 3
+        for g in range(PASSES):
+            for t in range(T):
+                regroup = nc.vector.tensor_copy if t < VECTOR_GROUPS else nc.scalar.copy
+                regroup(
+                    out=w_grouped[:, g, t].rearrange("q (e u) j -> q e u j", e=E),
+                    in_=w_raw[:, t, g].rearrange("q j (u e) -> q e u j", u=U),
+                )
+            nc.scalar.copy(
+                out=w_grouped[:, g, SHARED],
+                in_=w_raw[:, SHARED, g].rearrange("q j k -> q k j"),
+            )
+        for g in range(PASSES):
+            nc.vector.quantize_mx(
+                out=w_codes[:, g, 0 : T * UE].bitcast(FP8X4),
+                scales=w_scales[:, g, 0 : T * UE],
+                in_=w_grouped[:, g, 0:T].rearrange("q s k j -> q (s k j)"),
+            )
+            nc.vector.quantize_mx(
+                out=w_codes[:, g, T * UE : SOURCES * UE].bitcast(FP8X4),
+                scales=w_scales[:, g, T * UE : SOURCES * UE],
+                in_=w_grouped[:, g, SHARED].rearrange("q k j -> q (k j)"),
+            )
+
+        bias_cols = keep.tile([P, P], F32)
+        nc.vector.tensor_copy(out=bias_cols[:], in_=bias_ps[:])
+        bias_col_of = [t for t in range(T)] + [SHARED_ROW]
+
+        gates_exp(first_job)
+        gates_inverse(first_job)
+        gates_write(first_job)
+
+        x_grouped, x_codes, x_scales = {}, {}, {}
+        experts, shared_prod, own_prod = {}, {}, {}
+        sums_ps, sums_sb, share_parts = {}, {}, {}
+        stage_task, stage_share = {}, {}
+
+        def transpose_x(r, i):
+            if i == 0:
+                x_grouped[r] = work.tile(
+                    [P, PASSES, ROUND, P, PACK], BF16, align_bytes=64, name="x_grouped"
+                )
+            xt_ps = ps_xt.tile([P, PASSES, 2, P], F32)
+            for g in range(PASSES):
+                for h in range(2):
+                    nc.tensor.transpose(
+                        out=xt_ps[:, g, h, :],
+                        in_=x_tiles[r][:].bitcast(F32)[:, i, 2 * P * g + h : 2 * P * (g + 1) : 2],
+                        identity=ident[:],
+                    )
+            nc.scalar.copy(
+                out=x_grouped[r][:].bitcast(F32)[:, :, i, :, :],
+                in_=xt_ps[:].rearrange("q g h b -> q g b h"),
+            )
+
+        def quantize_x(r):
+            x_codes[r] = work.tile([P, PASSES, COLS], U32, align_bytes=64, name="x_codes")
+            x_scales[r] = work.tile([P, PASSES, COLS], U8, align_bytes=64, name="x_scales")
+            for g in range(PASSES):
+                nc.vector.quantize_mx(
+                    out=x_codes[r][:, g, :].bitcast(FP8X4),
+                    scales=x_scales[r][:, g, :],
+                    in_=x_grouped[r][:, g].rearrange("q i b j -> q (i b j)"),
+                )
+
+        def expert_group(r, group):
+            if group == SHARED:
+                experts[r] = work.tile([P, SOURCES, COLS], F32, name="experts")
+            columns = slice(group * UE, (group + 1) * UE)
+            y_ps = ps_y.tile([P, COLS], F32)
+            for g in range(PASSES):
+                nc.tensor.matmul_mx(
+                    out=y_ps[:],
+                    lhsT=w_codes[:, g, columns].bitcast(FP8X4),
+                    lhsT_scale=w_scales[:, g, columns],
+                    rhs=x_codes[r][:, g, :].bitcast(FP8X4),
+                    rhs_scale=x_scales[r][:, g, :],
+                    start=(g == 0),
+                    stop=(g == PASSES - 1),
+                )
+            nc.scalar.activation(
+                out=experts[r][:, group, :],
+                in_=y_ps[:],
+                func=ACT.Relu,
+                bias=bias_cols[:, bias_col_of[group] : bias_col_of[group] + 1],
+                scale=1.0,
+            )
+
+        def shared_products(r):
+            shared_ps = ps_misc.tile([P, ROUND, UE], F32, tag="misc")
+            for i in range(ROUND):
+                nc.tensor.transpose(
+                    out=shared_ps[:, i, :],
+                    in_=experts[r][:, SHARED, i * P : (i + 1) * P],
+                    identity=ident[:],
+                )
+            shared_sb = work.tile([P, ROUND, U, E], F32)
+            nc.scalar.copy(out=shared_sb[:].rearrange("b i u e -> b i (u e)"), in_=shared_ps[:])
+            shared_prod[r] = work.tile([P, ROUND, SOURCES, U, E], F32, name="shared_prod")
+            full = [P, ROUND, SOURCES, U, E]
+            nc.gpsimd.tensor_tensor(
+                out=shared_prod[r][:],
+                in0=shared_sb[:].unsqueeze(2).to_broadcast(full),
+                in1=gates_shared[:, r * ROUND : (r + 1) * ROUND].unsqueeze(3).to_broadcast(full),
+                op=ALU.mult,
+            )
+
+        def shared_reduce(r):
+            nc.vector.tensor_reduce(
+                out=shared_sums[r % 2][:, :, 0:SLOTS_USED],
+                in_=shared_prod[r][:].rearrange("b i o u e -> b i (o u) e"),
+                axis=AXIS_X,
+                op=ALU.add,
+            )
+
+        def own_products(r, i):
+            own_ps = ps_own.tile([P, E, T, U], F32)
+            for t in range(T):
+                nc.tensor.transpose(
+                    out=own_ps[:, :, t, :],
+                    in_=experts[r][:, t, i * P : (i + 1) * P],
+                    identity=ident[:],
+                )
+            own_prod[(r, i)] = prod.tile([P, E, 2, T, U], F32, name="own_prod")
+            full = [P, E, 2, T, U]
+            nc.vector.tensor_tensor(
+                out=own_prod[(r, i)][:],
+                in0=own_ps[:].unsqueeze(2).to_broadcast(full),
+                in1=gates_own[:, r * ROUND + i].unsqueeze(4).to_broadcast(full),
+                op=ALU.mult,
+            )
+
+        def sum_over_experts(r, i):
+            if i == 0:
+                sums_ps[r] = ps_misc.tile([P, ROUND, P], F32, tag="misc", name="sums_ps")
+            for e in range(E):
+                nc.tensor.matmul(
+                    out=sums_ps[r][:, i, :],
+                    lhsT=own_prod[(r, i)][:, e].rearrange("b h t u -> b (h t u)"),
+                    rhs=ident[:],
+                    is_transpose=True,
+                    start=(e == 0),
+                    stop=False,
+                )
+            nc.tensor.matmul(
+                out=sums_ps[r][:, i, :],
+                lhsT=shared_sums[r % 2][:, i, :],
+                rhs=ident[:],
+                is_transpose=True,
+                start=False,
+                stop=True,
+            )
+
+        def sums_out(r):
+            sums_sb[r] = work.tile([P, ROUND, P], F32, name="sums_sb")
+            nc.scalar.copy(out=sums_sb[r][:], in_=sums_ps[r][:])
+
+        def transpose_back(r):
+            back_ps = ps_misc.tile([P, ROUND, 2, T, U], F32, tag="misc")
+            for i in range(ROUND):
+                nc.tensor.transpose(
+                    out=back_ps[:, i].rearrange("b h t u -> b (h t u)"),
+                    in_=sums_sb[r][:, i, :],
+                    identity=ident[:],
+                )
+            batch = r // STORE_ROUNDS
+            if r % STORE_ROUNDS == 0:
+                stage_task[batch] = work.tile(
+                    [P, T, STORE_ROUNDS * ROUND, U], F32, name="stage_task"
+                )
+                stage_share[batch] = work.tile(
+                    [P, STORE_ROUNDS * ROUND, U], F32, name="stage_share"
+                )
+            at = (r % STORE_ROUNDS) * ROUND
+            nc.scalar.copy(
+                out=stage_task[batch][:, :, at : at + ROUND, :],
+                in_=back_ps[:, :, 0].rearrange("b i t u -> b t i u"),
+            )
+            share_parts[r] = work.tile([P, ROUND, T, U], F32, name="share_parts")
+            nc.scalar.copy(out=share_parts[r][:], in_=back_ps[:, :, 1])
+
+        def finish(r):
+            batch = r // STORE_ROUNDS
+            at = (r % STORE_ROUNDS) * ROUND
+            nc.vector.tensor_reduce(
+                out=stage_share[batch][:, at : at + ROUND, :],
+                in_=share_parts[r][:].rearrange("b i t u -> b i u t"),
+                axis=AXIS_X,
+                op=ALU.add,
+            )
+            if r % STORE_ROUNDS == STORE_ROUNDS - 1:
+                n0 = batch * STORE_ROUNDS * ROUND
+                n1 = n0 + STORE_ROUNDS * ROUND
+                nc.sync.dma_start(out=out_task_rows[:, :, n0:n1, :], in_=stage_task[batch][:])
+                nc.sync.dma_start(out=out_share_rows[:, n0:n1, :], in_=stage_share[batch][:])
+
+        def step(make, r, *which):
+            if 0 <= r < ROUNDS:
+                make(r, *which)
+
+        for s in range(-GATE_LEAD, ROUNDS + 2):
+            if s in gate_job_rows:
+                gate_jobs[s] = gate_job(*gate_job_rows[s])
+                gates_logits(gate_jobs[s])
+            if s - 1 in gate_jobs:
+                gates_subtract(gate_jobs[s - 1])
+            if s - 2 in gate_jobs:
+                gates_write(gate_jobs[s - 2])
+            step(own_products, s, 0)
+            step(own_products, s, 1)
+            step(expert_group, s + 1, SHARED)
+            step(transpose_back, s - 2)
+            step(quantize_x, s + 2)
+            step(shared_reduce, s)
+            for i in range(ROUND):
+                step(transpose_x, s + 3, i)
+                step(expert_group, s + 1, i)
+                if i == 0:
+                    step(shared_products, s + 1)
+                if i == 1 and s - 1 in gate_jobs:
+                    gates_exp(gate_jobs[s - 1])
+                if i + 1 in (2, 3):
+                    step(own_products, s, i + 1)
+                step(sum_over_experts, s - 1, i)
+            step(sums_out, s - 1)
+            if s in gate_jobs:
+                gates_top(gate_jobs[s])
+            if s - 1 in gate_jobs:
+                gates_inverse(gate_jobs[s - 1])
+            step(finish, s - 2)
+            if s + 3 >= 0:
+                step(load_x, s + 3 + X_AHEAD)

@@ -26,9 +26,8 @@ ROW_TILES = B // P
 ROUND = 4
 ROUNDS = ROW_TILES // ROUND
 COLS = ROUND * P
-GATE_CHUNK = 16
+GATE_CHUNK = 8
 STORE_ROUNDS = 4
-SLOTS_USED = SOURCES * U
 
 FLOPS = 2 * B * D * SOURCES * UE
 
@@ -39,50 +38,21 @@ def tile_plelayer_pa_t_kernel(
     nc = tc.nc
     with ExitStack() as ctx:
         keep = ctx.enter_context(tc.tile_pool(name="keep", bufs=1))
-        gate_tmp = ctx.enter_context(tc.tile_pool(name="gate_tmp", bufs=2))
+        gate_tmp = ctx.enter_context(tc.tile_pool(name="gate_tmp", bufs=3))
         x_pool = ctx.enter_context(tc.tile_pool(name="x_pool", bufs=3))
         work = ctx.enter_context(tc.tile_pool(name="work", bufs=2))
+        words = ctx.enter_context(tc.tile_pool(name="words", bufs=3))
+        sums_pool = ctx.enter_context(tc.tile_pool(name="sums_pool", bufs=5))
         prod = ctx.enter_context(tc.tile_pool(name="prod", bufs=2 * ROUND))
-        ps_xt = ctx.enter_context(tc.psum_pool(name="ps_xt", bufs=2))
         ps_y = ctx.enter_context(tc.psum_pool(name="ps_y", bufs=2))
-        ps_own = ctx.enter_context(tc.psum_pool(name="ps_own", bufs=2))
-        ps_misc = ctx.enter_context(tc.psum_pool(name="ps_misc", bufs=2))
+        ps_own = ctx.enter_context(tc.psum_pool(name="ps_own", bufs=4))
+        ps_sums = ctx.enter_context(tc.psum_pool(name="ps_sums", bufs=1))
+        ps_misc = ctx.enter_context(tc.psum_pool(name="ps_misc", bufs=1))
         ctx.enter_context(tc.manual_schedule())
 
         x_rows = x.rearrange("(p n) k -> p n k", n=ROW_TILES)
         out_task_rows = out_0.rearrange("t (p n) u -> p t n u", n=ROW_TILES)
         out_share_rows = out_1.rearrange("(p n) u -> p n u", n=ROW_TILES)
-
-        SHARED_ROW = 32
-        bias_rows = keep.tile([P, UE], BF16)
-        nc.scalar.dma_start(out=bias_rows[0:T, :], in_=eb0.rearrange("t u e -> t (u e)"))
-        nc.scalar.dma_start(
-            out=bias_rows[SHARED_ROW : SHARED_ROW + 1, :],
-            in_=ebs0.rearrange("(o u) e -> o (u e)", o=1),
-        )
-        gate_bias_task = keep.tile([P, T, G_TASK], BF16)
-        nc.scalar.dma_start(
-            out=gate_bias_task[:].rearrange("p t k -> p (t k)"),
-            in_=gb0.rearrange("t k -> (t k)").partition_broadcast(P),
-        )
-        gate_bias_share = keep.tile([P, G_SHARE], BF16)
-        nc.scalar.dma_start(out=gate_bias_share[:], in_=gbs.partition_broadcast(P))
-        pre_task = keep.tile([P, T, ROW_TILES, G_TASK], BF16)
-        pre_share = keep.tile([P, ROW_TILES, G_SHARE], BF16)
-        pre_task_rows = gate_pre0.rearrange("t (p n) k -> p t n k", n=ROW_TILES)
-        pre_share_rows = sgate_pre.rearrange("(p n) k -> p n k", n=ROW_TILES)
-        nc.scalar.dma_start(out=pre_task[:, :, 0:ROUND, :], in_=pre_task_rows[:, :, 0:ROUND, :])
-        nc.scalar.dma_start(out=pre_share[:, 0:ROUND, :], in_=pre_share_rows[:, 0:ROUND, :])
-        w_raw = keep.tile([P, SOURCES, PASSES, PACK, UE], BF16)
-        for t in range(T):
-            nc.sync.dma_start(
-                out=w_raw[:, t],
-                in_=ew0[t].rearrange("(g q j) u e -> q g j (u e)", g=PASSES, j=PACK),
-            )
-        nc.sync.dma_start(
-            out=w_raw[:, SHARED],
-            in_=ews0.rearrange("(g q j) u e -> q g j (u e)", g=PASSES, j=PACK),
-        )
 
         x_tiles = {}
 
@@ -93,199 +63,209 @@ def tile_plelayer_pa_t_kernel(
 
         X_AHEAD = 3
         load_x(0)
+        w_raw = keep.tile([P, SOURCES, PASSES, PACK, UE], BF16)
         nc.sync.dma_start(
-            out=pre_task[:, :, ROUND:ROW_TILES, :], in_=pre_task_rows[:, :, ROUND:ROW_TILES, :]
+            out=w_raw[:, SHARED],
+            in_=ews0.rearrange("(g q j) u e -> q g j (u e)", g=PASSES, j=PACK),
         )
-        nc.sync.dma_start(
-            out=pre_share[:, ROUND:ROW_TILES, :], in_=pre_share_rows[:, ROUND:ROW_TILES, :]
+        for t in range(T):
+            nc.sync.dma_start(
+                out=w_raw[:, t],
+                in_=ew0[t].rearrange("(g q j) u e -> q g j (u e)", g=PASSES, j=PACK),
+            )
+        PRE_FIRST = 2 * ROUND
+        pre_task = keep.tile([P, T, ROW_TILES, G_TASK], BF16)
+        pre_share = keep.tile([P, ROW_TILES, G_SHARE], BF16)
+        pre_task_rows = gate_pre0.rearrange("t (p n) k -> p t n k", n=ROW_TILES)
+        pre_share_rows = sgate_pre.rearrange("(p n) k -> p n k", n=ROW_TILES)
+        nc.scalar.dma_start(
+            out=pre_task[:, :, 0:PRE_FIRST, :], in_=pre_task_rows[:, :, 0:PRE_FIRST, :]
+        )
+        nc.scalar.dma_start(out=pre_share[:, 0:PRE_FIRST, :], in_=pre_share_rows[:, 0:PRE_FIRST, :])
+        gate_bias_task = keep.tile([P, T, G_TASK], BF16)
+        nc.scalar.dma_start(
+            out=gate_bias_task[:].rearrange("p t k -> p (t k)"),
+            in_=gb0.rearrange("t k -> (t k)").partition_broadcast(P),
+        )
+        gate_bias_share = keep.tile([P, G_SHARE], BF16)
+        nc.scalar.dma_start(out=gate_bias_share[:], in_=gbs.partition_broadcast(P))
+        neg_bias_task = keep.tile([P, T, G_TASK], BF16)
+        neg_bias_share = keep.tile([P, G_SHARE], BF16)
+        SHARED_ROW = 32
+        bias_rows = keep.tile([P, UE], BF16)
+        nc.scalar.dma_start(out=bias_rows[0:T, :], in_=eb0.rearrange("t u e -> t (u e)"))
+        nc.scalar.dma_start(
+            out=bias_rows[SHARED_ROW : SHARED_ROW + 1, :],
+            in_=ebs0.rearrange("(o u) e -> o (u e)", o=1),
         )
         for r in range(1, X_AHEAD):
             load_x(r)
+        nc.sync.dma_start(
+            out=pre_task[:, :, PRE_FIRST:, :], in_=pre_task_rows[:, :, PRE_FIRST:, :]
+        )
+        nc.sync.dma_start(out=pre_share[:, PRE_FIRST:, :], in_=pre_share_rows[:, PRE_FIRST:, :])
 
         ident = keep.tile([P, P], F32)
         make_identity(nc, ident[:])
 
-        gates_own = keep.tile([P, ROW_TILES, E, 2, T], F32)
-        gates_shared = keep.tile([P, ROW_TILES, SOURCES, E], F32)
+        gates_own = keep.tile([P, ROW_TILES, 2, T, E], F32)
+        gates_other = keep.tile([P, ROW_TILES, SOURCES, E], F32)
 
-        def gate_job(first_row_tile, count):
-            task_tile = gate_tmp.tile([P, T, GATE_CHUNK, G_TASK], F32)
+        def gates_logits(k):
+            task_tile = gate_tmp.tile([P, GATE_CHUNK, T, G_TASK], F32)
             share_tile = gate_tmp.tile([P, GATE_CHUNK, G_SHARE], F32)
-            task_top = gate_tmp.tile([P, T, GATE_CHUNK], F32)
-            share_top = gate_tmp.tile([P, GATE_CHUNK], F32)
-            task_sum = gate_tmp.tile([P, T, GATE_CHUNK], F32)
-            share_sum = gate_tmp.tile([P, GATE_CHUNK], F32)
-            task_inv = gate_tmp.tile([P, T, GATE_CHUNK], F32)
-            share_inv = gate_tmp.tile([P, GATE_CHUNK], F32)
-            return {
-                "rows": slice(first_row_tile, first_row_tile + count),
-                "count": count,
-                "task": task_tile[:, :, 0:count, :],
-                "share": share_tile[:, 0:count, :],
-                "task_top": task_top[:, :, 0:count],
-                "share_top": share_top[:, 0:count],
-                "task_sum": task_sum[:, :, 0:count],
-                "share_sum": share_sum[:, 0:count],
-                "task_inv": task_inv[:, :, 0:count],
-                "share_inv": share_inv[:, 0:count],
-            }
-
-        def gates_logits(job):
-            rows, count = job["rows"], job["count"]
+            neg_top = gate_tmp.tile([P, GATE_CHUNK, SOURCES], F32)
+            sums = gate_tmp.tile([P, GATE_CHUNK, SOURCES], F32)
+            inv = gate_tmp.tile([P, GATE_CHUNK, SOURCES], F32)
+            gate_tiles[k] = (task_tile, share_tile, neg_top, sums, inv)
+            rows = slice(k * GATE_CHUNK, (k + 1) * GATE_CHUNK)
             nc.gpsimd.tensor_tensor(
-                out=job["task"],
-                in0=pre_task[:, :, rows, :],
-                in1=gate_bias_task[:].unsqueeze(2).to_broadcast([P, T, count, G_TASK]),
-                op=ALU.add,
-            )
-            nc.gpsimd.tensor_tensor(
-                out=job["share"],
-                in0=pre_share[:, rows, :],
-                in1=gate_bias_share[:].unsqueeze(1).to_broadcast([P, count, G_SHARE]),
-                op=ALU.add,
-            )
-
-        def gates_top(job):
-            nc.vector.tensor_reduce(out=job["task_top"], in_=job["task"], axis=AXIS_X, op=ALU.max)
-            nc.vector.tensor_reduce(out=job["share_top"], in_=job["share"], axis=AXIS_X, op=ALU.max)
-
-        def gates_subtract(job):
-            count = job["count"]
-            nc.gpsimd.tensor_tensor(
-                out=job["task"],
-                in0=job["task"],
-                in1=job["task_top"].unsqueeze(3).to_broadcast([P, T, count, G_TASK]),
+                out=task_tile[:],
+                in0=neg_bias_task[:].unsqueeze(1).to_broadcast([P, GATE_CHUNK, T, G_TASK]),
+                in1=pre_task[:, :, rows, :].rearrange("p t n k -> p n t k"),
                 op=ALU.subtract,
             )
             nc.gpsimd.tensor_tensor(
-                out=job["share"],
-                in0=job["share"],
-                in1=job["share_top"].unsqueeze(2).to_broadcast([P, count, G_SHARE]),
+                out=share_tile[:],
+                in0=neg_bias_share[:].unsqueeze(1).to_broadcast([P, GATE_CHUNK, G_SHARE]),
+                in1=pre_share[:, rows, :],
                 op=ALU.subtract,
             )
 
-        def gates_exp(job):
-            nc.scalar.activation(out=job["task"], in_=job["task"], func=ACT.Exp)
-            nc.scalar.activation(out=job["share"], in_=job["share"], func=ACT.Exp)
+        def gates_top(r):
+            task_tile, share_tile, neg_top, sums, inv = gate_tiles[r // 2]
+            part = slice(r % 2 * ROUND, (r % 2 + 1) * ROUND)
+            nc.vector.tensor_reduce(
+                out=neg_top[:, part, 0:T], in_=task_tile[:, part], axis=AXIS_X, op=ALU.min
+            )
+            nc.vector.tensor_reduce(
+                out=neg_top[:, part, SHARED], in_=share_tile[:, part], axis=AXIS_X, op=ALU.min
+            )
 
-        def gates_inverse(job):
-            nc.vector.tensor_reduce(out=job["task_sum"], in_=job["task"], axis=AXIS_X, op=ALU.add)
-            nc.vector.tensor_reduce(out=job["share_sum"], in_=job["share"], axis=AXIS_X, op=ALU.add)
-            nc.vector.reciprocal(out=job["task_inv"], in_=job["task_sum"])
-            nc.vector.reciprocal(out=job["share_inv"], in_=job["share_sum"])
+        def gates_exp(r, i):
+            task_tile, share_tile, neg_top, sums, inv = gate_tiles[r // 2]
+            n = r % 2 * ROUND + i
+            for o in range(SOURCES):
+                values = task_tile[:, n, o, :] if o < T else share_tile[:, n, :]
+                nc.scalar.activation(
+                    out=values,
+                    in_=values,
+                    func=ACT.Exp,
+                    bias=neg_top[:, n, o : o + 1],
+                    scale=-1.0,
+                    accum_out=sums[:, n, o : o + 1],
+                )
 
-        def gates_write(job):
-            rows, count = job["rows"], job["count"]
-            task_inv_nt = job["task_inv"].rearrange("p t n -> p n t")
+        def gates_inverse(r):
+            task_tile, share_tile, neg_top, sums, inv = gate_tiles[r // 2]
+            part = slice(r % 2 * ROUND, (r % 2 + 1) * ROUND)
+            nc.vector.reciprocal(out=inv[:, part], in_=sums[:, part])
+
+        def gates_write(r, count):
+            task_tile, share_tile, neg_top, sums, inv = gate_tiles[r // 2]
+            size = count * ROUND
+            rows = slice(r * ROUND, r * ROUND + size)
+            part = slice(r % 2 * ROUND, r % 2 * ROUND + size)
+            for gates, first in ((gates_own[:, rows, 0], 0), (gates_other[:, rows, 0:T], E)):
+                nc.gpsimd.tensor_tensor(
+                    out=gates,
+                    in0=task_tile[:, part, :, first : first + E],
+                    in1=inv[:, part, 0:T].unsqueeze(3).to_broadcast([P, size, T, E]),
+                    op=ALU.mult,
+                )
             nc.gpsimd.tensor_tensor(
-                out=gates_shared[:, rows, 0:T, :],
-                in0=job["task"][:, :, :, E:G_TASK].rearrange("p t n e -> p n t e"),
-                in1=task_inv_nt.unsqueeze(3).to_broadcast([P, count, T, E]),
+                out=gates_own[:, rows, 1].rearrange("p n t e -> p n (t e)"),
+                in0=share_tile[:, part, 0 : T * E],
+                in1=inv[:, part, SHARED].unsqueeze(2).to_broadcast([P, size, T * E]),
                 op=ALU.mult,
             )
             nc.gpsimd.tensor_tensor(
-                out=gates_shared[:, rows, SHARED, :],
-                in0=job["share"][:, :, T * E : G_SHARE],
-                in1=job["share_inv"].unsqueeze(2).to_broadcast([P, count, E]),
-                op=ALU.mult,
-            )
-            nc.gpsimd.tensor_tensor(
-                out=gates_own[:, rows, :, 0, :],
-                in0=job["task"][:, :, :, 0:E].rearrange("p t n e -> p n e t"),
-                in1=task_inv_nt.unsqueeze(2).to_broadcast([P, count, E, T]),
-                op=ALU.mult,
-            )
-            nc.gpsimd.tensor_tensor(
-                out=gates_own[:, rows, :, 1, :],
-                in0=job["share"][:, :, 0 : T * E].rearrange("p n (t e) -> p n e t", t=T),
-                in1=job["share_inv"].unsqueeze(2).unsqueeze(3).to_broadcast([P, count, E, T]),
+                out=gates_other[:, rows, SHARED],
+                in0=share_tile[:, part, T * E : G_SHARE],
+                in1=inv[:, part, SHARED].unsqueeze(2).to_broadcast([P, size, E]),
                 op=ALU.mult,
             )
 
-        GATE_LEAD = 3
-        gate_job_rows = {1 - GATE_LEAD: (ROUND, GATE_CHUNK - ROUND)}
-        for chunk in range(1, ROW_TILES // GATE_CHUNK):
-            gate_job_rows[chunk * GATE_CHUNK // ROUND - GATE_LEAD] = (chunk * GATE_CHUNK, GATE_CHUNK)
-        gate_jobs = {}
-        first_job = gate_job(0, ROUND)
+        gate_tiles = {}
 
-        shared_sum_a = keep.tile([P, ROUND, P], F32)
-        shared_sum_b = keep.tile([P, ROUND, P], F32)
-        shared_sums = [shared_sum_a, shared_sum_b]
+        shared_sums = {}
         bias_square = keep.tile([P, P], F32)
         nc.vector.memset(bias_square[:], 0.0)
-        for shared_sum in shared_sums:
-            nc.vector.memset(shared_sum[:], 0.0)
-
-        nc.vector.tensor_copy(
-            out=bias_square[0:T, :].rearrange("t (e u) -> t e u", e=E),
-            in_=bias_rows[0:T, :].rearrange("t (u e) -> t e u", e=E),
-        )
-        nc.vector.tensor_copy(
-            out=bias_square[SHARED_ROW : SHARED_ROW + 1, :],
-            in_=bias_rows[SHARED_ROW : SHARED_ROW + 1, :],
-        )
-        bias_ps = ps_misc.tile([P, P], F32, tag="misc")
-        nc.tensor.transpose(out=bias_ps[:], in_=bias_square[:], identity=ident[:])
-
-        gates_logits(first_job)
-        gates_top(first_job)
-        gates_subtract(first_job)
-
-        w_grouped = keep.tile([P, PASSES, SOURCES, UE, PACK], BF16, align_bytes=64)
-        w_codes = keep.tile([P, PASSES, SOURCES * UE], U32, align_bytes=64)
-        w_scales = keep.tile([P, PASSES, SOURCES * UE], U8, align_bytes=64)
-        VECTOR_GROUPS = 3
-        for g in range(PASSES):
-            for t in range(T):
-                regroup = nc.vector.tensor_copy if t < VECTOR_GROUPS else nc.scalar.copy
-                regroup(
-                    out=w_grouped[:, g, t].rearrange("q (e u) j -> q e u j", e=E),
-                    in_=w_raw[:, t, g].rearrange("q j (u e) -> q e u j", u=U),
-                )
-            nc.scalar.copy(
-                out=w_grouped[:, g, SHARED],
-                in_=w_raw[:, SHARED, g].rearrange("q j k -> q k j"),
-            )
-        for g in range(PASSES):
-            nc.vector.quantize_mx(
-                out=w_codes[:, g, 0 : T * UE].bitcast(FP8X4),
-                scales=w_scales[:, g, 0 : T * UE],
-                in_=w_grouped[:, g, 0:T].rearrange("q s k j -> q (s k j)"),
-            )
-            nc.vector.quantize_mx(
-                out=w_codes[:, g, T * UE : SOURCES * UE].bitcast(FP8X4),
-                scales=w_scales[:, g, T * UE : SOURCES * UE],
-                in_=w_grouped[:, g, SHARED].rearrange("q k j -> q (k j)"),
-            )
 
         bias_cols = keep.tile([P, P], F32)
-        nc.vector.tensor_copy(out=bias_cols[:], in_=bias_ps[:])
         bias_col_of = [t for t in range(T)] + [SHARED_ROW]
 
-        gates_exp(first_job)
-        gates_inverse(first_job)
-        gates_write(first_job)
+        def expert_biases():
+            nc.vector.tensor_copy(
+                out=bias_square[0:T, :].rearrange("t (e u) -> t e u", e=E),
+                in_=bias_rows[0:T, :].rearrange("t (u e) -> t e u", e=E),
+            )
+            nc.vector.tensor_copy(
+                out=bias_square[SHARED_ROW : SHARED_ROW + 1, :],
+                in_=bias_rows[SHARED_ROW : SHARED_ROW + 1, :],
+            )
+            bias_ps = ps_misc.tile([P, P], F32, tag="misc")
+            nc.tensor.transpose(out=bias_ps[:], in_=bias_square[:], identity=ident[:])
+            nc.vector.tensor_copy(out=bias_cols[:], in_=bias_ps[:])
 
-        x_grouped, x_codes, x_scales = {}, {}, {}
+        w_grouped = keep.tile([P, SOURCES, PASSES, UE, PACK], BF16, align_bytes=64)
+        w_codes = keep.tile([P, SOURCES, PASSES, UE], U32, align_bytes=64)
+        w_scales = keep.tile([P, SOURCES, PASSES, UE], U8, align_bytes=64)
+
+        def regroup_weights(group):
+            for g in range(PASSES):
+                if group == SHARED:
+                    nc.vector.tensor_copy(
+                        out=w_grouped[:, SHARED, g],
+                        in_=w_raw[:, SHARED, g].rearrange("q j k -> q k j"),
+                    )
+                else:
+                    nc.vector.tensor_copy(
+                        out=w_grouped[:, group, g].rearrange("q (e u) j -> q e u j", e=E),
+                        in_=w_raw[:, group, g].rearrange("q j (u e) -> q e u j", u=U),
+                    )
+
+        def quantize_weights(group):
+            nc.vector.quantize_mx(
+                out=w_codes[:, group].rearrange("q g k -> q (g k)").bitcast(FP8X4),
+                scales=w_scales[:, group].rearrange("q g k -> q (g k)"),
+                in_=w_grouped[:, group].rearrange("q g k j -> q (g k j)"),
+            )
+
+        x_words, x_grouped, x_codes, x_scales = {}, {}, {}, {}
         experts, shared_prod, own_prod = {}, {}, {}
-        sums_ps, sums_sb, share_parts = {}, {}, {}
+        sums_ps, sums_sb, back, own_rows_ps = {}, {}, {}, {}
+        shared_rows_ps, shared_rows_sb, share_sums = {}, {}, {}
+        SCALAR_COLS = UE - E
         stage_task, stage_share = {}, {}
 
-        def transpose_x(r, i):
+        UNORDERED_ROUNDS = range(4)
+
+        def order_x(r, i):
+            if r in UNORDERED_ROUNDS:
+                return
+            x_words[(r, i)] = words.tile([P, PASSES, 2, P], F32, name="x_words")
+            nc.scalar.copy(
+                out=x_words[(r, i)][:],
+                in_=x_tiles[r][:].bitcast(F32)[:, i, :].rearrange(
+                    "b (g q h) -> b g h q", g=PASSES, h=2
+                ),
+            )
+
+        def transpose_x(r, i, pool=ps_own, tag="own_ps", copy=nc.scalar.copy):
             if i == 0:
                 x_grouped[r] = work.tile(
                     [P, PASSES, ROUND, P, PACK], BF16, align_bytes=64, name="x_grouped"
                 )
-            xt_ps = ps_xt.tile([P, PASSES, 2, P], F32)
+            xt_ps = pool.tile([P, PASSES, 2, P], F32, tag=tag)
             for g in range(PASSES):
                 for h in range(2):
-                    nc.tensor.transpose(
-                        out=xt_ps[:, g, h, :],
-                        in_=x_tiles[r][:].bitcast(F32)[:, i, 2 * P * g + h : 2 * P * (g + 1) : 2],
-                        identity=ident[:],
-                    )
-            nc.scalar.copy(
+                    if r in UNORDERED_ROUNDS:
+                        half = x_tiles[r][:].bitcast(F32)[:, i, 2 * P * g + h : 2 * P * (g + 1) : 2]
+                    else:
+                        half = x_words[(r, i)][:, g, h, :]
+                    nc.tensor.transpose(out=xt_ps[:, g, h, :], in_=half, identity=ident[:])
+            copy(
                 out=x_grouped[r][:].bitcast(F32)[:, :, i, :, :],
                 in_=xt_ps[:].rearrange("q g h b -> q g b h"),
             )
@@ -303,13 +283,12 @@ def tile_plelayer_pa_t_kernel(
         def expert_group(r, group):
             if group == SHARED:
                 experts[r] = work.tile([P, SOURCES, COLS], F32, name="experts")
-            columns = slice(group * UE, (group + 1) * UE)
-            y_ps = ps_y.tile([P, COLS], F32)
+            y_ps = ps_y.tile([P, COLS], F32, tag="y_ps")
             for g in range(PASSES):
                 nc.tensor.matmul_mx(
                     out=y_ps[:],
-                    lhsT=w_codes[:, g, columns].bitcast(FP8X4),
-                    lhsT_scale=w_scales[:, g, columns],
+                    lhsT=w_codes[:, group, g].bitcast(FP8X4),
+                    lhsT_scale=w_scales[:, group, g],
                     rhs=x_codes[r][:, g, :].bitcast(FP8X4),
                     rhs_scale=x_scales[r][:, g, :],
                     start=(g == 0),
@@ -323,53 +302,72 @@ def tile_plelayer_pa_t_kernel(
                 scale=1.0,
             )
 
-        def shared_products(r):
+        def shared_rows(r):
             shared_ps = ps_misc.tile([P, ROUND, UE], F32, tag="misc")
+            shared_rows_ps[r] = shared_ps
             for i in range(ROUND):
                 nc.tensor.transpose(
                     out=shared_ps[:, i, :],
                     in_=experts[r][:, SHARED, i * P : (i + 1) * P],
                     identity=ident[:],
                 )
-            shared_sb = work.tile([P, ROUND, U, E], F32)
-            nc.scalar.copy(out=shared_sb[:].rearrange("b i u e -> b i (u e)"), in_=shared_ps[:])
+            shared_rows_sb[r] = work.tile([P, ROUND, UE], F32, name="shared_rows_sb")
+            nc.scalar.copy(
+                out=shared_rows_sb[r][:, :, 0:SCALAR_COLS], in_=shared_ps[:, :, 0:SCALAR_COLS]
+            )
+
+        def shared_rest(r):
+            nc.vector.tensor_copy(
+                out=shared_rows_sb[r][:, :, SCALAR_COLS:UE],
+                in_=shared_rows_ps[r][:, :, SCALAR_COLS:UE],
+            )
+
+        def shared_products(r):
             shared_prod[r] = work.tile([P, ROUND, SOURCES, U, E], F32, name="shared_prod")
             full = [P, ROUND, SOURCES, U, E]
             nc.gpsimd.tensor_tensor(
                 out=shared_prod[r][:],
-                in0=shared_sb[:].unsqueeze(2).to_broadcast(full),
-                in1=gates_shared[:, r * ROUND : (r + 1) * ROUND].unsqueeze(3).to_broadcast(full),
+                in0=shared_rows_sb[r][:].rearrange("b i (u e) -> b i u e", e=E).unsqueeze(2).to_broadcast(full),
+                in1=gates_other[:, r * ROUND : (r + 1) * ROUND]
+                .unsqueeze(3)
+                .to_broadcast(full),
                 op=ALU.mult,
             )
 
         def shared_reduce(r):
+            shared_sums[r] = sums_pool.tile([P, ROUND, SOURCES, U], F32, name="shared_sum")
             nc.vector.tensor_reduce(
-                out=shared_sums[r % 2][:, :, 0:SLOTS_USED],
+                out=shared_sums[r][:].rearrange("b i o u -> b i (o u)"),
                 in_=shared_prod[r][:].rearrange("b i o u e -> b i (o u) e"),
                 axis=AXIS_X,
                 op=ALU.add,
             )
 
-        def own_products(r, i):
-            own_ps = ps_own.tile([P, E, T, U], F32)
+        def own_rows(r, i):
+            own_ps = ps_own.tile([P, E, T, U], F32, tag="own_ps")
+            own_rows_ps[(r, i)] = own_ps
             for t in range(T):
                 nc.tensor.transpose(
                     out=own_ps[:, :, t, :],
                     in_=experts[r][:, t, i * P : (i + 1) * P],
                     identity=ident[:],
                 )
+
+        def own_products(r, i):
+            own_ps = own_rows_ps[(r, i)]
             own_prod[(r, i)] = prod.tile([P, E, 2, T, U], F32, name="own_prod")
+            own_gates = gates_own[:, r * ROUND + i].rearrange("p h t e -> p e h t")
             full = [P, E, 2, T, U]
             nc.vector.tensor_tensor(
                 out=own_prod[(r, i)][:],
                 in0=own_ps[:].unsqueeze(2).to_broadcast(full),
-                in1=gates_own[:, r * ROUND + i].unsqueeze(4).to_broadcast(full),
+                in1=own_gates.unsqueeze(4).to_broadcast(full),
                 op=ALU.mult,
             )
 
         def sum_over_experts(r, i):
             if i == 0:
-                sums_ps[r] = ps_misc.tile([P, ROUND, P], F32, tag="misc", name="sums_ps")
+                sums_ps[r] = ps_sums.tile([P, ROUND, P], F32, name="sums_ps")
             for e in range(E):
                 nc.tensor.matmul(
                     out=sums_ps[r][:, i, :],
@@ -377,16 +375,8 @@ def tile_plelayer_pa_t_kernel(
                     rhs=ident[:],
                     is_transpose=True,
                     start=(e == 0),
-                    stop=False,
+                    stop=(e == E - 1),
                 )
-            nc.tensor.matmul(
-                out=sums_ps[r][:, i, :],
-                lhsT=shared_sums[r % 2][:, i, :],
-                rhs=ident[:],
-                is_transpose=True,
-                start=False,
-                stop=True,
-            )
 
         def sums_out(r):
             sums_sb[r] = work.tile([P, ROUND, P], F32, name="sums_sb")
@@ -394,12 +384,16 @@ def tile_plelayer_pa_t_kernel(
 
         def transpose_back(r):
             back_ps = ps_misc.tile([P, ROUND, 2, T, U], F32, tag="misc")
+            back[r] = back_ps
             for i in range(ROUND):
                 nc.tensor.transpose(
                     out=back_ps[:, i].rearrange("b h t u -> b (h t u)"),
                     in_=sums_sb[r][:, i, :],
                     identity=ident[:],
                 )
+
+        def finish(r):
+            back_ps = back[r]
             batch = r // STORE_ROUNDS
             if r % STORE_ROUNDS == 0:
                 stage_task[batch] = work.tile(
@@ -409,20 +403,27 @@ def tile_plelayer_pa_t_kernel(
                     [P, STORE_ROUNDS * ROUND, U], F32, name="stage_share"
                 )
             at = (r % STORE_ROUNDS) * ROUND
-            nc.scalar.copy(
-                out=stage_task[batch][:, :, at : at + ROUND, :],
-                in_=back_ps[:, :, 0].rearrange("b i t u -> b t i u"),
+            share_sums[r] = work.tile([P, ROUND, U], F32, name="share_sum")
+            nc.vector.tensor_reduce(
+                out=share_sums[r][:],
+                in_=back_ps[:, :, 1].rearrange("b i t u -> b i u t"),
+                axis=AXIS_X,
+                op=ALU.add,
             )
-            share_parts[r] = work.tile([P, ROUND, T, U], F32, name="share_parts")
-            nc.scalar.copy(out=share_parts[r][:], in_=back_ps[:, :, 1])
+            nc.vector.tensor_tensor(
+                out=stage_task[batch][:, :, at : at + ROUND, :].rearrange("b t i u -> b i t u"),
+                in0=back_ps[:, :, 0],
+                in1=shared_sums[r][:, :, 0:T],
+                op=ALU.add,
+            )
 
-        def finish(r):
+        def finish_share(r):
             batch = r // STORE_ROUNDS
             at = (r % STORE_ROUNDS) * ROUND
-            nc.vector.tensor_reduce(
+            nc.gpsimd.tensor_tensor(
                 out=stage_share[batch][:, at : at + ROUND, :],
-                in_=share_parts[r][:].rearrange("b i t u -> b i u t"),
-                axis=AXIS_X,
+                in0=share_sums[r][:],
+                in1=shared_sums[r][:, :, SHARED],
                 op=ALU.add,
             )
             if r % STORE_ROUNDS == STORE_ROUNDS - 1:
@@ -435,35 +436,102 @@ def tile_plelayer_pa_t_kernel(
             if 0 <= r < ROUNDS:
                 make(r, *which)
 
-        for s in range(-GATE_LEAD, ROUNDS + 2):
-            if s in gate_job_rows:
-                gate_jobs[s] = gate_job(*gate_job_rows[s])
-                gates_logits(gate_jobs[s])
-            if s - 1 in gate_jobs:
-                gates_subtract(gate_jobs[s - 1])
-            if s - 2 in gate_jobs:
-                gates_write(gate_jobs[s - 2])
-            step(own_products, s, 0)
-            step(own_products, s, 1)
+        nc.vector.tensor_scalar_mul(out=neg_bias_task[:], in0=gate_bias_task[:], scalar1=-1.0)
+        nc.vector.tensor_scalar_mul(out=neg_bias_share[:], in0=gate_bias_share[:], scalar1=-1.0)
+        gates_logits(0)
+        for i in range(ROUND):
+            transpose_x(0, i, ps_own, "own_ps")
+        regroup_weights(SHARED)
+        quantize_weights(SHARED)
+        gates_top(0)
+        for i in range(ROUND):
+            gates_exp(0, i)
+        regroup_weights(0)
+        quantize_weights(0)
+        quantize_x(0)
+        expert_biases()
+        expert_group(0, SHARED)
+        gates_inverse(0)
+        gates_write(0, 1)
+        for t in range(1, T):
+            regroup_weights(t)
+            quantize_weights(t)
+        gates_top(1)
+        gates_logits(1)
+        expert_group(0, 0)
+        shared_rows(0)
+        transpose_x(1, 0, ps_own, "own_ps")
+        transpose_x(1, 1, ps_own, "own_ps")
+        expert_group(0, 1)
+        expert_group(0, 2)
+        transpose_x(1, 2, ps_own, "own_ps")
+        transpose_x(1, 3, ps_own, "own_ps")
+        expert_group(0, 3)
+        for i in range(ROUND):
+            gates_exp(1, i)
+        quantize_x(1)
+        gates_inverse(1)
+        shared_rest(0)
+        shared_products(0)
+        gates_write(1, 1)
+        gates_logits(2)
+        gates_top(2)
+        gates_top(3)
+        for i in range(ROUND):
+            transpose_x(2, i, ps_y, "y_ps")
+        for r in range(X_AHEAD, 2 * X_AHEAD):
+            load_x(r)
+        order_x(3, 0)
+
+        for s in range(ROUNDS + 3):
+            exp_rounds = [2, 3] if s == 0 else [s + 3]
             step(expert_group, s + 1, SHARED)
-            step(transpose_back, s - 2)
+            step(order_x, s + 3, 1)
+            for r in exp_rounds:
+                step(gates_exp, r, 0)
+            step(own_rows, s, 0)
+            step(own_rows, s, 1)
+            step(finish, s - 3)
+            step(own_products, s, 0)
+            step(sum_over_experts, s - 1, 0)
+            step(own_products, s, 1)
+            step(expert_group, s + 1, 0)
+            for r in exp_rounds:
+                step(gates_exp, r, 1)
             step(quantize_x, s + 2)
+            step(shared_rows, s + 1)
+            step(shared_rest, s + 1)
+            step(shared_products, s + 1)
+            step(own_rows, s, 2)
+            step(own_products, s, 2)
+            step(transpose_x, s + 3, 0)
+            step(order_x, s + 3, 2)
+            for r in exp_rounds:
+                step(gates_exp, r, 2)
+            step(expert_group, s + 1, 1)
+            step(own_rows, s, 3)
+            step(own_products, s, 3)
+            step(sum_over_experts, s - 1, 1)
+            step(transpose_x, s + 3, 1)
+            step(order_x, s + 3, 3)
+            for r in exp_rounds:
+                step(gates_exp, r, 3)
+            step(expert_group, s + 1, 2)
             step(shared_reduce, s)
-            for i in range(ROUND):
-                step(transpose_x, s + 3, i)
-                step(expert_group, s + 1, i)
-                if i == 0:
-                    step(shared_products, s + 1)
-                if i == 1 and s - 1 in gate_jobs:
-                    gates_exp(gate_jobs[s - 1])
-                if i + 1 in (2, 3):
-                    step(own_products, s, i + 1)
-                step(sum_over_experts, s - 1, i)
+            step(sum_over_experts, s - 1, 2)
+            step(transpose_x, s + 3, 2)
+            step(order_x, s + 4, 0)
+            step(expert_group, s + 1, 3)
+            step(sum_over_experts, s - 1, 3)
             step(sums_out, s - 1)
-            if s in gate_jobs:
-                gates_top(gate_jobs[s])
-            if s - 1 in gate_jobs:
-                gates_inverse(gate_jobs[s - 1])
-            step(finish, s - 2)
-            if s + 3 >= 0:
-                step(load_x, s + 3 + X_AHEAD)
+            step(transpose_x, s + 3, 3)
+            step(transpose_back, s - 2)
+            step(finish_share, s - 3)
+            for r in exp_rounds:
+                step(gates_inverse, r)
+            step(gates_top, s + 4)
+            if s % 2 == 0:
+                step(gates_write, s + 2, 2)
+            elif s + 5 < ROUNDS:
+                gates_logits((s + 5) // 2)
+            step(load_x, s + 3 + X_AHEAD)

@@ -27,7 +27,7 @@ ROUND = 4
 ROUNDS = ROW_TILES // ROUND
 COLS = ROUND * P
 GATE_CHUNK = 8
-STORE_ROUNDS = 4
+STORE_ROUNDS = 2
 
 FLOPS = 2 * B * D * SOURCES * UE
 
@@ -73,6 +73,13 @@ def tile_plelayer_pa_t_kernel(
                 out=w_raw[:, t],
                 in_=ew0[t].rearrange("(g q j) u e -> q g j (u e)", g=PASSES, j=PACK),
             )
+        gate_bias_task = keep.tile([P, T, G_TASK], BF16)
+        nc.scalar.dma_start(
+            out=gate_bias_task[:].rearrange("p t k -> p (t k)"),
+            in_=gb0.rearrange("t k -> (t k)").partition_broadcast(P),
+        )
+        gate_bias_share = keep.tile([P, G_SHARE], BF16)
+        nc.scalar.dma_start(out=gate_bias_share[:], in_=gbs.partition_broadcast(P))
         PRE_FIRST = 2 * ROUND
         pre_task = keep.tile([P, T, ROW_TILES, G_TASK], BF16)
         pre_share = keep.tile([P, ROW_TILES, G_SHARE], BF16)
@@ -82,13 +89,6 @@ def tile_plelayer_pa_t_kernel(
             out=pre_task[:, :, 0:PRE_FIRST, :], in_=pre_task_rows[:, :, 0:PRE_FIRST, :]
         )
         nc.scalar.dma_start(out=pre_share[:, 0:PRE_FIRST, :], in_=pre_share_rows[:, 0:PRE_FIRST, :])
-        gate_bias_task = keep.tile([P, T, G_TASK], BF16)
-        nc.scalar.dma_start(
-            out=gate_bias_task[:].rearrange("p t k -> p (t k)"),
-            in_=gb0.rearrange("t k -> (t k)").partition_broadcast(P),
-        )
-        gate_bias_share = keep.tile([P, G_SHARE], BF16)
-        nc.scalar.dma_start(out=gate_bias_share[:], in_=gbs.partition_broadcast(P))
         neg_bias_task = keep.tile([P, T, G_TASK], BF16)
         neg_bias_share = keep.tile([P, G_SHARE], BF16)
         SHARED_ROW = 32
@@ -206,7 +206,7 @@ def tile_plelayer_pa_t_kernel(
             )
             bias_ps = ps_misc.tile([P, P], F32, tag="misc")
             nc.tensor.transpose(out=bias_ps[:], in_=bias_square[:], identity=ident[:])
-            nc.vector.tensor_copy(out=bias_cols[:], in_=bias_ps[:])
+            return bias_ps
 
         w_grouped = keep.tile([P, SOURCES, PASSES, UE, PACK], BF16, align_bytes=64)
         w_codes = keep.tile([P, SOURCES, PASSES, UE], U32, align_bytes=64)
@@ -383,7 +383,8 @@ def tile_plelayer_pa_t_kernel(
             nc.scalar.copy(out=sums_sb[r][:], in_=sums_ps[r][:])
 
         def transpose_back(r):
-            back_ps = ps_misc.tile([P, ROUND, 2, T, U], F32, tag="misc")
+            pool, tag = (ps_misc, "misc") if r < ROUNDS - 2 else (ps_own, "own_ps")
+            back_ps = pool.tile([P, ROUND, 2, T, U], F32, tag=tag, name="back_ps")
             back[r] = back_ps
             for i in range(ROUND):
                 nc.tensor.transpose(
@@ -440,45 +441,51 @@ def tile_plelayer_pa_t_kernel(
         nc.vector.tensor_scalar_mul(out=neg_bias_share[:], in0=gate_bias_share[:], scalar1=-1.0)
         gates_logits(0)
         for i in range(ROUND):
-            transpose_x(0, i, ps_own, "own_ps")
+            transpose_x(0, i)
         regroup_weights(SHARED)
         quantize_weights(SHARED)
+        bias_ps = expert_biases()
         gates_top(0)
         for i in range(ROUND):
             gates_exp(0, i)
         regroup_weights(0)
+        nc.vector.tensor_copy(out=bias_cols[:], in_=bias_ps[:])
         quantize_weights(0)
         quantize_x(0)
-        expert_biases()
         expert_group(0, SHARED)
         gates_inverse(0)
         gates_write(0, 1)
-        for t in range(1, T):
-            regroup_weights(t)
-            quantize_weights(t)
+        regroup_weights(1)
+        quantize_weights(1)
+        expert_group(0, 0)
         gates_top(1)
         gates_logits(1)
-        expert_group(0, 0)
         shared_rows(0)
-        transpose_x(1, 0, ps_own, "own_ps")
-        transpose_x(1, 1, ps_own, "own_ps")
+        transpose_x(1, 0)
+        transpose_x(1, 1)
+        regroup_weights(2)
+        quantize_weights(2)
         expert_group(0, 1)
+        regroup_weights(3)
+        quantize_weights(3)
         expert_group(0, 2)
-        transpose_x(1, 2, ps_own, "own_ps")
-        transpose_x(1, 3, ps_own, "own_ps")
+        transpose_x(1, 2, copy=nc.vector.tensor_copy)
+        transpose_x(1, 3, copy=nc.vector.tensor_copy)
         expert_group(0, 3)
-        for i in range(ROUND):
-            gates_exp(1, i)
         quantize_x(1)
-        gates_inverse(1)
         shared_rest(0)
         shared_products(0)
-        gates_write(1, 1)
-        gates_logits(2)
         gates_top(2)
         gates_top(3)
+        transpose_x(2, 0)
+        transpose_x(2, 1)
         for i in range(ROUND):
-            transpose_x(2, i, ps_y, "y_ps")
+            gates_exp(1, i)
+        transpose_x(2, 2)
+        transpose_x(2, 3)
+        gates_inverse(1)
+        gates_write(1, 1)
+        gates_logits(2)
         for r in range(X_AHEAD, 2 * X_AHEAD):
             load_x(r)
         order_x(3, 0)

@@ -493,6 +493,7 @@ def tile_plelayer_pa_t_kernel(
         for s in range(ROUNDS + 3):
             exp_rounds = [2, 3] if s == 0 else [s + 3]
             step(expert_group, s + 1, SHARED)
+            step(expert_group, s + 1, 0)
             step(order_x, s + 3, 1)
             for r in exp_rounds:
                 step(gates_exp, r, 0)
@@ -502,9 +503,6 @@ def tile_plelayer_pa_t_kernel(
             step(own_products, s, 0)
             step(sum_over_experts, s - 1, 0)
             step(own_products, s, 1)
-            step(expert_group, s + 1, 0)
-            for r in exp_rounds:
-                step(gates_exp, r, 1)
             step(quantize_x, s + 2)
             step(shared_rows, s + 1)
             step(shared_rest, s + 1)
@@ -514,8 +512,11 @@ def tile_plelayer_pa_t_kernel(
             step(transpose_x, s + 3, 0)
             step(order_x, s + 3, 2)
             for r in exp_rounds:
-                step(gates_exp, r, 2)
+                step(gates_exp, r, 1)
             step(expert_group, s + 1, 1)
+            step(expert_group, s + 1, 2)
+            for r in exp_rounds:
+                step(gates_exp, r, 2)
             step(own_rows, s, 3)
             step(own_products, s, 3)
             step(sum_over_experts, s - 1, 1)
@@ -523,12 +524,11 @@ def tile_plelayer_pa_t_kernel(
             step(order_x, s + 3, 3)
             for r in exp_rounds:
                 step(gates_exp, r, 3)
-            step(expert_group, s + 1, 2)
-            step(shared_reduce, s)
             step(sum_over_experts, s - 1, 2)
+            step(expert_group, s + 1, 3)
+            step(shared_reduce, s)
             step(transpose_x, s + 3, 2)
             step(order_x, s + 4, 0)
-            step(expert_group, s + 1, 3)
             step(sum_over_experts, s - 1, 3)
             step(sums_out, s - 1)
             step(transpose_x, s + 3, 3)

@@ -38,11 +38,10 @@ def tile_plelayer_pa_t_kernel(
     nc = tc.nc
     with ExitStack() as ctx:
         keep = ctx.enter_context(tc.tile_pool(name="keep", bufs=1))
-        gate_tmp = ctx.enter_context(tc.tile_pool(name="gate_tmp", bufs=3))
+        gate_tmp = ctx.enter_context(tc.tile_pool(name="gate_tmp", bufs=2))
         x_pool = ctx.enter_context(tc.tile_pool(name="x_pool", bufs=3))
         work = ctx.enter_context(tc.tile_pool(name="work", bufs=2))
         words = ctx.enter_context(tc.tile_pool(name="words", bufs=3))
-        sums_pool = ctx.enter_context(tc.tile_pool(name="sums_pool", bufs=5))
         prod = ctx.enter_context(tc.tile_pool(name="prod", bufs=2 * ROUND))
         ps_y = ctx.enter_context(tc.psum_pool(name="ps_y", bufs=2))
         ps_own = ctx.enter_context(tc.psum_pool(name="ps_own", bufs=4))
@@ -54,15 +53,48 @@ def tile_plelayer_pa_t_kernel(
         out_task_rows = out_0.rearrange("t (p n) u -> p t n u", n=ROW_TILES)
         out_share_rows = out_1.rearrange("(p n) u -> p n u", n=ROW_TILES)
 
+        bias_row = keep.tile([P, T * G_TASK + G_SHARE], BF16)
+        nc.vector.memset(bias_row[:], 0.0)
+        nc.scalar.dma_start(
+            out=bias_row[0:1, 0 : T * G_TASK],
+            in_=gb0.rearrange("t k -> (t k)").rearrange("(o c) -> o c", o=1),
+        )
+        nc.scalar.dma_start(
+            out=bias_row[0:1, T * G_TASK :], in_=gbs.rearrange("(o c) -> o c", o=1)
+        )
+        pre_task = keep.tile([P, T, ROW_TILES, G_TASK], BF16)
+        pre_share = keep.tile([P, ROW_TILES, G_SHARE], BF16)
+        pre_task_rows = gate_pre0.rearrange("t (p n) k -> p t n k", n=ROW_TILES)
+        pre_share_rows = sgate_pre.rearrange("(p n) k -> p n k", n=ROW_TILES)
+
+        def load_gates(queue, first, count):
+            rows = slice(first * ROUND, (first + count) * ROUND)
+            queue.dma_start(out=pre_task[:, :, rows, :], in_=pre_task_rows[:, :, rows, :])
+            queue.dma_start(out=pre_share[:, rows, :], in_=pre_share_rows[:, rows, :])
+
+        load_gates(nc.scalar, 0, 2)
+        SHARED_ROW = 32
+        bias_rows = keep.tile([P, UE], BF16)
+        nc.scalar.dma_start(out=bias_rows[0:T, :], in_=eb0.rearrange("t u e -> t (u e)"))
+        nc.scalar.dma_start(
+            out=bias_rows[SHARED_ROW : SHARED_ROW + 1, :],
+            in_=ebs0.rearrange("(o u) e -> o (u e)", o=1),
+        )
+
         x_tiles = {}
 
-        def load_x(r):
+        def load_x(r, pieces=1):
             x_sb = x_pool.tile([P, ROUND, D], BF16)
-            nc.sync.dma_start(out=x_sb[:], in_=x_rows[:, r * ROUND : (r + 1) * ROUND, :])
+            size = ROUND // pieces
+            for first in range(0, ROUND, size):
+                nc.sync.dma_start(
+                    out=x_sb[:, first : first + size, :],
+                    in_=x_rows[:, r * ROUND + first : r * ROUND + first + size, :],
+                )
             x_tiles[r] = x_sb
 
         X_AHEAD = 3
-        load_x(0)
+        load_x(0, ROUND)
         w_raw = keep.tile([P, SOURCES, PASSES, PACK, UE], BF16)
         nc.sync.dma_start(
             out=w_raw[:, SHARED],
@@ -73,122 +105,119 @@ def tile_plelayer_pa_t_kernel(
                 out=w_raw[:, t],
                 in_=ew0[t].rearrange("(g q j) u e -> q g j (u e)", g=PASSES, j=PACK),
             )
-        gate_bias_task = keep.tile([P, T, G_TASK], BF16)
-        nc.scalar.dma_start(
-            out=gate_bias_task[:].rearrange("p t k -> p (t k)"),
-            in_=gb0.rearrange("t k -> (t k)").partition_broadcast(P),
-        )
-        gate_bias_share = keep.tile([P, G_SHARE], BF16)
-        nc.scalar.dma_start(out=gate_bias_share[:], in_=gbs.partition_broadcast(P))
-        PRE_FIRST = 2 * ROUND
-        pre_task = keep.tile([P, T, ROW_TILES, G_TASK], BF16)
-        pre_share = keep.tile([P, ROW_TILES, G_SHARE], BF16)
-        pre_task_rows = gate_pre0.rearrange("t (p n) k -> p t n k", n=ROW_TILES)
-        pre_share_rows = sgate_pre.rearrange("(p n) k -> p n k", n=ROW_TILES)
-        nc.scalar.dma_start(
-            out=pre_task[:, :, 0:PRE_FIRST, :], in_=pre_task_rows[:, :, 0:PRE_FIRST, :]
-        )
-        nc.scalar.dma_start(out=pre_share[:, 0:PRE_FIRST, :], in_=pre_share_rows[:, 0:PRE_FIRST, :])
-        neg_bias_task = keep.tile([P, T, G_TASK], BF16)
-        neg_bias_share = keep.tile([P, G_SHARE], BF16)
-        SHARED_ROW = 32
-        bias_rows = keep.tile([P, UE], BF16)
-        nc.scalar.dma_start(out=bias_rows[0:T, :], in_=eb0.rearrange("t u e -> t (u e)"))
-        nc.scalar.dma_start(
-            out=bias_rows[SHARED_ROW : SHARED_ROW + 1, :],
-            in_=ebs0.rearrange("(o u) e -> o (u e)", o=1),
-        )
-        for r in range(1, X_AHEAD):
-            load_x(r)
-        nc.sync.dma_start(
-            out=pre_task[:, :, PRE_FIRST:, :], in_=pre_task_rows[:, :, PRE_FIRST:, :]
-        )
-        nc.sync.dma_start(out=pre_share[:, PRE_FIRST:, :], in_=pre_share_rows[:, PRE_FIRST:, :])
+        load_x(1, 2)
+        load_x(2)
+        load_gates(nc.sync, 2, 2)
+        load_gates(nc.sync, 4, ROUNDS - 4)
 
         ident = keep.tile([P, P], F32)
         make_identity(nc, ident[:])
 
-        gates_own = keep.tile([P, ROW_TILES, 2, T, E], F32)
-        gates_other = keep.tile([P, ROW_TILES, SOURCES, E], F32)
+        RUN = E
+        OWN_STEP, OTHER_STEP = 2 * RUN, 4 * RUN
+        GATE_ROW = SOURCES * OTHER_STEP
+        gates = keep.tile([P, ROW_TILES * GATE_ROW + 2 * OTHER_STEP], F32)
+        gate_inv = keep.tile([P, ROW_TILES, SOURCES], F32)
+
+        def own_gates(n):
+            row = gates[:, n * GATE_ROW : n * GATE_ROW + 2 * T * OWN_STEP]
+            return row.rearrange("p (j c) -> p j c", c=OWN_STEP)[:, :, RUN:]
+
+        def other_gates(n, count):
+            first = n * GATE_ROW + OTHER_STEP
+            rows = gates[:, first : first + count * GATE_ROW]
+            return rows.rearrange("p (o c) -> p o c", c=OTHER_STEP)[:, :, 0:RUN]
+
+        ones = keep.tile([P, P], BF16)
+        nc.vector.memset(ones[:], 1.0)
+        neg_bias = keep.tile([P, T * G_TASK + G_SHARE], BF16)
+        neg_bias_task = neg_bias[:, 0 : T * G_TASK].rearrange("p (t k) -> p t k", t=T)
+        neg_bias_share = neg_bias[:, T * G_TASK :]
+
+        def gate_biases():
+            spread_ps = ps_misc.tile([P, T * G_TASK + G_SHARE], F32, tag="misc")
+            nc.tensor.matmul(
+                out=spread_ps[:], lhsT=ones[:], rhs=bias_row[:], start=True, stop=True
+            )
+            nc.vector.tensor_scalar_mul(out=neg_bias[:], in0=spread_ps[:], scalar1=-1.0)
 
         def gates_logits(k):
             task_tile = gate_tmp.tile([P, GATE_CHUNK, T, G_TASK], F32)
             share_tile = gate_tmp.tile([P, GATE_CHUNK, G_SHARE], F32)
-            neg_top = gate_tmp.tile([P, GATE_CHUNK, SOURCES], F32)
-            sums = gate_tmp.tile([P, GATE_CHUNK, SOURCES], F32)
-            inv = gate_tmp.tile([P, GATE_CHUNK, SOURCES], F32)
-            gate_tiles[k] = (task_tile, share_tile, neg_top, sums, inv)
+            logits[k] = (task_tile, share_tile)
             rows = slice(k * GATE_CHUNK, (k + 1) * GATE_CHUNK)
             nc.gpsimd.tensor_tensor(
                 out=task_tile[:],
-                in0=neg_bias_task[:].unsqueeze(1).to_broadcast([P, GATE_CHUNK, T, G_TASK]),
+                in0=neg_bias_task.unsqueeze(1).to_broadcast([P, GATE_CHUNK, T, G_TASK]),
                 in1=pre_task[:, :, rows, :].rearrange("p t n k -> p n t k"),
                 op=ALU.subtract,
             )
             nc.gpsimd.tensor_tensor(
                 out=share_tile[:],
-                in0=neg_bias_share[:].unsqueeze(1).to_broadcast([P, GATE_CHUNK, G_SHARE]),
+                in0=neg_bias_share.unsqueeze(1).to_broadcast([P, GATE_CHUNK, G_SHARE]),
                 in1=pre_share[:, rows, :],
                 op=ALU.subtract,
             )
 
         def gates_top(r):
-            task_tile, share_tile, neg_top, sums, inv = gate_tiles[r // 2]
+            task_tile, share_tile = logits[r // 2]
             part = slice(r % 2 * ROUND, (r % 2 + 1) * ROUND)
+            neg_top[r] = gate_tmp.tile([P, ROUND, SOURCES], F32, name="neg_top")
             nc.vector.tensor_reduce(
-                out=neg_top[:, part, 0:T], in_=task_tile[:, part], axis=AXIS_X, op=ALU.min
+                out=neg_top[r][:, :, 0:T], in_=task_tile[:, part], axis=AXIS_X, op=ALU.min
             )
             nc.vector.tensor_reduce(
-                out=neg_top[:, part, SHARED], in_=share_tile[:, part], axis=AXIS_X, op=ALU.min
+                out=neg_top[r][:, :, SHARED], in_=share_tile[:, part], axis=AXIS_X, op=ALU.min
             )
 
         def gates_exp(r, i):
-            task_tile, share_tile, neg_top, sums, inv = gate_tiles[r // 2]
-            n = r % 2 * ROUND + i
-            for o in range(SOURCES):
-                values = task_tile[:, n, o, :] if o < T else share_tile[:, n, :]
+            task_tile, share_tile = logits[r // 2]
+            at = r % 2 * ROUND + i
+            n = r * ROUND + i
+
+            def exponentials(out, in_, o, part):
                 nc.scalar.activation(
-                    out=values,
-                    in_=values,
+                    out=out,
+                    in_=in_,
                     func=ACT.Exp,
-                    bias=neg_top[:, n, o : o + 1],
+                    bias=neg_top[r][:, i, o : o + 1],
                     scale=-1.0,
-                    accum_out=sums[:, n, o : o + 1],
+                    accum_out=gate_sums[:, n, o, part : part + 1],
                 )
 
-        def gates_inverse(r):
-            task_tile, share_tile, neg_top, sums, inv = gate_tiles[r // 2]
-            part = slice(r % 2 * ROUND, (r % 2 + 1) * ROUND)
-            nc.vector.reciprocal(out=inv[:, part], in_=sums[:, part])
-
-        def gates_write(r, count):
-            task_tile, share_tile, neg_top, sums, inv = gate_tiles[r // 2]
-            size = count * ROUND
-            rows = slice(r * ROUND, r * ROUND + size)
-            part = slice(r % 2 * ROUND, r % 2 * ROUND + size)
-            for gates, first in ((gates_own[:, rows, 0], 0), (gates_other[:, rows, 0:T], E)):
-                nc.gpsimd.tensor_tensor(
-                    out=gates,
-                    in0=task_tile[:, part, :, first : first + E],
-                    in1=inv[:, part, 0:T].unsqueeze(3).to_broadcast([P, size, T, E]),
-                    op=ALU.mult,
+            for t in range(T):
+                own = n * GATE_ROW + t * OWN_STEP + RUN
+                step = n * GATE_ROW + (t + 1) * OTHER_STEP - own
+                runs = gates[:, own : own + 2 * step].rearrange("p (k c) -> p k c", k=2)
+                exponentials(
+                    runs[:, :, 0:RUN], task_tile[:, at, t, :].rearrange("p (k e) -> p k e", k=2), t, 0
                 )
-            nc.gpsimd.tensor_tensor(
-                out=gates_own[:, rows, 1].rearrange("p n t e -> p n (t e)"),
-                in0=share_tile[:, part, 0 : T * E],
-                in1=inv[:, part, SHARED].unsqueeze(2).to_broadcast([P, size, T * E]),
-                op=ALU.mult,
+            exponentials(
+                own_gates(n)[:, T:, :],
+                share_tile[:, at, 0 : T * E].rearrange("p (t e) -> p t e", t=T),
+                SHARED,
+                0,
             )
-            nc.gpsimd.tensor_tensor(
-                out=gates_other[:, rows, SHARED],
-                in0=share_tile[:, part, T * E : G_SHARE],
-                in1=inv[:, part, SHARED].unsqueeze(2).to_broadcast([P, size, E]),
-                op=ALU.mult,
+            exponentials(
+                other_gates(n, 1)[:, SHARED, :], share_tile[:, at, T * E : G_SHARE], SHARED, 1
             )
 
-        gate_tiles = {}
+        def gates_inverse(r, count):
+            rows = slice(r * ROUND, (r + count) * ROUND)
+            nc.vector.tensor_reduce(
+                out=gate_inv[:, rows, :], in_=gate_sums[:, rows], axis=AXIS_X, op=ALU.add
+            )
+            nc.vector.reciprocal(out=gate_inv[:, rows, :], in_=gate_inv[:, rows, :])
 
-        shared_sums = {}
+        logits, neg_top = {}, {}
+        gate_sums = keep.tile([P, ROW_TILES, SOURCES, 2], F32)
+        nc.vector.memset(gate_sums[:], 0.0)
+
+        shared_sum_a = keep.tile([P, ROUND, P], F32)
+        shared_sum_b = keep.tile([P, ROUND, P], F32)
+        shared_sums = [shared_sum_a, shared_sum_b]
+        for shared_sum in shared_sums:
+            nc.gpsimd.memset(shared_sum[:], 0.0)
         bias_square = keep.tile([P, P], F32)
         nc.vector.memset(bias_square[:], 0.0)
 
@@ -212,15 +241,15 @@ def tile_plelayer_pa_t_kernel(
         w_codes = keep.tile([P, SOURCES, PASSES, UE], U32, align_bytes=64)
         w_scales = keep.tile([P, SOURCES, PASSES, UE], U8, align_bytes=64)
 
-        def regroup_weights(group):
+        def regroup_weights(group, copy=nc.vector.tensor_copy):
             for g in range(PASSES):
                 if group == SHARED:
-                    nc.vector.tensor_copy(
+                    copy(
                         out=w_grouped[:, SHARED, g],
                         in_=w_raw[:, SHARED, g].rearrange("q j k -> q k j"),
                     )
                 else:
-                    nc.vector.tensor_copy(
+                    copy(
                         out=w_grouped[:, group, g].rearrange("q (e u) j -> q e u j", e=E),
                         in_=w_raw[:, group, g].rearrange("q j (u e) -> q e u j", u=U),
                     )
@@ -241,8 +270,11 @@ def tile_plelayer_pa_t_kernel(
 
         UNORDERED_ROUNDS = range(4)
 
+        def unordered(r, i):
+            return r in UNORDERED_ROUNDS or i == 3
+
         def order_x(r, i):
-            if r in UNORDERED_ROUNDS:
+            if unordered(r, i):
                 return
             x_words[(r, i)] = words.tile([P, PASSES, 2, P], F32, name="x_words")
             nc.scalar.copy(
@@ -260,7 +292,7 @@ def tile_plelayer_pa_t_kernel(
             xt_ps = pool.tile([P, PASSES, 2, P], F32, tag=tag)
             for g in range(PASSES):
                 for h in range(2):
-                    if r in UNORDERED_ROUNDS:
+                    if unordered(r, i):
                         half = x_tiles[r][:].bitcast(F32)[:, i, 2 * P * g + h : 2 * P * (g + 1) : 2]
                     else:
                         half = x_words[(r, i)][:, g, h, :]
@@ -273,12 +305,11 @@ def tile_plelayer_pa_t_kernel(
         def quantize_x(r):
             x_codes[r] = work.tile([P, PASSES, COLS], U32, align_bytes=64, name="x_codes")
             x_scales[r] = work.tile([P, PASSES, COLS], U8, align_bytes=64, name="x_scales")
-            for g in range(PASSES):
-                nc.vector.quantize_mx(
-                    out=x_codes[r][:, g, :].bitcast(FP8X4),
-                    scales=x_scales[r][:, g, :],
-                    in_=x_grouped[r][:, g].rearrange("q i b j -> q (i b j)"),
-                )
+            nc.vector.quantize_mx(
+                out=x_codes[r][:].rearrange("q g c -> q (g c)").bitcast(FP8X4),
+                scales=x_scales[r][:].rearrange("q g c -> q (g c)"),
+                in_=x_grouped[r][:].rearrange("q g i b j -> q (g i b j)"),
+            )
 
         def expert_group(r, group):
             if group == SHARED:
@@ -328,16 +359,16 @@ def tile_plelayer_pa_t_kernel(
             nc.gpsimd.tensor_tensor(
                 out=shared_prod[r][:],
                 in0=shared_rows_sb[r][:].rearrange("b i (u e) -> b i u e", e=E).unsqueeze(2).to_broadcast(full),
-                in1=gates_other[:, r * ROUND : (r + 1) * ROUND]
+                in1=other_gates(r * ROUND, ROUND)
+                .rearrange("p (i o) e -> p i o e", i=ROUND)
                 .unsqueeze(3)
                 .to_broadcast(full),
                 op=ALU.mult,
             )
 
         def shared_reduce(r):
-            shared_sums[r] = sums_pool.tile([P, ROUND, SOURCES, U], F32, name="shared_sum")
             nc.vector.tensor_reduce(
-                out=shared_sums[r][:].rearrange("b i o u -> b i (o u)"),
+                out=shared_sums[r % 2][:, :, 0 : SOURCES * U],
                 in_=shared_prod[r][:].rearrange("b i o u e -> b i (o u) e"),
                 axis=AXIS_X,
                 op=ALU.add,
@@ -356,12 +387,12 @@ def tile_plelayer_pa_t_kernel(
         def own_products(r, i):
             own_ps = own_rows_ps[(r, i)]
             own_prod[(r, i)] = prod.tile([P, E, 2, T, U], F32, name="own_prod")
-            own_gates = gates_own[:, r * ROUND + i].rearrange("p h t e -> p e h t")
+            gate_runs = own_gates(r * ROUND + i).rearrange("p (h t) e -> p e h t", h=2)
             full = [P, E, 2, T, U]
             nc.vector.tensor_tensor(
                 out=own_prod[(r, i)][:],
                 in0=own_ps[:].unsqueeze(2).to_broadcast(full),
-                in1=own_gates.unsqueeze(4).to_broadcast(full),
+                in1=gate_runs.unsqueeze(4).to_broadcast(full),
                 op=ALU.mult,
             )
 
@@ -375,8 +406,16 @@ def tile_plelayer_pa_t_kernel(
                     rhs=ident[:],
                     is_transpose=True,
                     start=(e == 0),
-                    stop=(e == E - 1),
+                    stop=False,
                 )
+            nc.tensor.matmul(
+                out=sums_ps[r][:, i, :],
+                lhsT=shared_sums[r % 2][:, i, :],
+                rhs=ident[:],
+                is_transpose=True,
+                start=False,
+                stop=True,
+            )
 
         def sums_out(r):
             sums_sb[r] = work.tile([P, ROUND, P], F32, name="sums_sb")
@@ -384,17 +423,15 @@ def tile_plelayer_pa_t_kernel(
 
         def transpose_back(r):
             pool, tag = (ps_misc, "misc") if r < ROUNDS - 2 else (ps_own, "own_ps")
-            back_ps = pool.tile([P, ROUND, 2, T, U], F32, tag=tag, name="back_ps")
-            back[r] = back_ps
+            back[r] = pool.tile([P, ROUND, 2, T, U], F32, tag=tag, name="back_ps")
             for i in range(ROUND):
                 nc.tensor.transpose(
-                    out=back_ps[:, i].rearrange("b h t u -> b (h t u)"),
+                    out=back[r][:, i].rearrange("b h t u -> b (h t u)"),
                     in_=sums_sb[r][:, i, :],
                     identity=ident[:],
                 )
 
         def finish(r):
-            back_ps = back[r]
             batch = r // STORE_ROUNDS
             if r % STORE_ROUNDS == 0:
                 stage_task[batch] = work.tile(
@@ -404,29 +441,31 @@ def tile_plelayer_pa_t_kernel(
                     [P, STORE_ROUNDS * ROUND, U], F32, name="stage_share"
                 )
             at = (r % STORE_ROUNDS) * ROUND
-            share_sums[r] = work.tile([P, ROUND, U], F32, name="share_sum")
-            nc.vector.tensor_reduce(
-                out=share_sums[r][:],
-                in_=back_ps[:, :, 1].rearrange("b i t u -> b i u t"),
-                axis=AXIS_X,
-                op=ALU.add,
-            )
+            rows = slice(r * ROUND, (r + 1) * ROUND)
             nc.vector.tensor_tensor(
                 out=stage_task[batch][:, :, at : at + ROUND, :].rearrange("b t i u -> b i t u"),
-                in0=back_ps[:, :, 0],
-                in1=shared_sums[r][:, :, 0:T],
+                in0=back[r][:, :, 0],
+                in1=gate_inv[:, rows, 0:T].unsqueeze(3).to_broadcast([P, ROUND, T, U]),
+                op=ALU.mult,
+            )
+            nc.vector.tensor_reduce(
+                out=stage_share[batch][:, at : at + ROUND, :],
+                in_=back[r][:, :, 1].rearrange("b i t u -> b i u t"),
+                axis=AXIS_X,
                 op=ALU.add,
             )
 
         def finish_share(r):
             batch = r // STORE_ROUNDS
             at = (r % STORE_ROUNDS) * ROUND
-            nc.gpsimd.tensor_tensor(
-                out=stage_share[batch][:, at : at + ROUND, :],
-                in0=share_sums[r][:],
-                in1=shared_sums[r][:, :, SHARED],
-                op=ALU.add,
-            )
+            for i in range(ROUND):
+                n = r * ROUND + i
+                nc.scalar.activation(
+                    out=stage_share[batch][:, at + i, :],
+                    in_=stage_share[batch][:, at + i, :],
+                    func=ACT.Copy,
+                    scale=gate_inv[:, n, SHARED : SHARED + 1],
+                )
             if r % STORE_ROUNDS == STORE_ROUNDS - 1:
                 n0 = batch * STORE_ROUNDS * ROUND
                 n1 = n0 + STORE_ROUNDS * ROUND
@@ -437,8 +476,7 @@ def tile_plelayer_pa_t_kernel(
             if 0 <= r < ROUNDS:
                 make(r, *which)
 
-        nc.vector.tensor_scalar_mul(out=neg_bias_task[:], in0=gate_bias_task[:], scalar1=-1.0)
-        nc.vector.tensor_scalar_mul(out=neg_bias_share[:], in0=gate_bias_share[:], scalar1=-1.0)
+        gate_biases()
         gates_logits(0)
         for i in range(ROUND):
             transpose_x(0, i)
@@ -448,55 +486,47 @@ def tile_plelayer_pa_t_kernel(
         gates_top(0)
         for i in range(ROUND):
             gates_exp(0, i)
-        regroup_weights(0)
         nc.vector.tensor_copy(out=bias_cols[:], in_=bias_ps[:])
-        quantize_weights(0)
         quantize_x(0)
         expert_group(0, SHARED)
-        gates_inverse(0)
-        gates_write(0, 1)
+        regroup_weights(0)
+        quantize_weights(0)
+        expert_group(0, 0)
         regroup_weights(1)
         quantize_weights(1)
-        expert_group(0, 0)
-        gates_top(1)
-        gates_logits(1)
         shared_rows(0)
         transpose_x(1, 0)
         transpose_x(1, 1)
+        expert_group(0, 1)
         regroup_weights(2)
         quantize_weights(2)
-        expert_group(0, 1)
+        expert_group(0, 2)
         regroup_weights(3)
         quantize_weights(3)
-        expert_group(0, 2)
         transpose_x(1, 2, copy=nc.vector.tensor_copy)
         transpose_x(1, 3, copy=nc.vector.tensor_copy)
         expert_group(0, 3)
+        gates_top(1)
+        gates_logits(1)
         quantize_x(1)
         shared_rest(0)
-        shared_products(0)
         gates_top(2)
-        gates_top(3)
+        shared_products(0)
         transpose_x(2, 0)
         transpose_x(2, 1)
         for i in range(ROUND):
             gates_exp(1, i)
         transpose_x(2, 2)
         transpose_x(2, 3)
-        gates_inverse(1)
-        gates_write(1, 1)
-        gates_logits(2)
         for r in range(X_AHEAD, 2 * X_AHEAD):
             load_x(r)
         order_x(3, 0)
 
         for s in range(ROUNDS + 3):
-            exp_rounds = [2, 3] if s == 0 else [s + 3]
             step(expert_group, s + 1, SHARED)
             step(expert_group, s + 1, 0)
             step(order_x, s + 3, 1)
-            for r in exp_rounds:
-                step(gates_exp, r, 0)
+            step(gates_exp, s + 2, 0)
             step(own_rows, s, 0)
             step(own_rows, s, 1)
             step(finish, s - 3)
@@ -507,23 +537,21 @@ def tile_plelayer_pa_t_kernel(
             step(shared_rows, s + 1)
             step(shared_rest, s + 1)
             step(shared_products, s + 1)
+            step(gates_exp, s + 2, 1)
             step(own_rows, s, 2)
             step(own_products, s, 2)
             step(transpose_x, s + 3, 0)
             step(order_x, s + 3, 2)
-            for r in exp_rounds:
-                step(gates_exp, r, 1)
+            step(finish_share, s - 3)
             step(expert_group, s + 1, 1)
             step(expert_group, s + 1, 2)
-            for r in exp_rounds:
-                step(gates_exp, r, 2)
+            step(gates_exp, s + 2, 2)
             step(own_rows, s, 3)
             step(own_products, s, 3)
             step(sum_over_experts, s - 1, 1)
             step(transpose_x, s + 3, 1)
             step(order_x, s + 3, 3)
-            for r in exp_rounds:
-                step(gates_exp, r, 3)
+            step(gates_exp, s + 2, 3)
             step(sum_over_experts, s - 1, 2)
             step(expert_group, s + 1, 3)
             step(shared_reduce, s)
@@ -533,12 +561,9 @@ def tile_plelayer_pa_t_kernel(
             step(sums_out, s - 1)
             step(transpose_x, s + 3, 3)
             step(transpose_back, s - 2)
-            step(finish_share, s - 3)
-            for r in exp_rounds:
-                step(gates_inverse, r)
-            step(gates_top, s + 4)
+            step(gates_top, s + 3)
             if s % 2 == 0:
-                step(gates_write, s + 2, 2)
-            elif s + 5 < ROUNDS:
-                gates_logits((s + 5) // 2)
+                step(gates_inverse, s, 2)
+                if s + 4 < ROUNDS:
+                    gates_logits((s + 4) // 2)
             step(load_x, s + 3 + X_AHEAD)

@@ -107,8 +107,7 @@ def tile_plelayer_pa_t_kernel(
             )
         load_x(1, 2)
         load_x(2)
-        load_gates(nc.sync, 2, 2)
-        load_gates(nc.sync, 4, ROUNDS - 4)
+        load_gates(nc.sync, 2, ROUNDS - 2)
 
         ident = keep.tile([P, P], F32)
         make_identity(nc, ident[:])
@@ -159,15 +158,14 @@ def tile_plelayer_pa_t_kernel(
                 op=ALU.subtract,
             )
 
-        def gates_top(r):
-            task_tile, share_tile = logits[r // 2]
-            part = slice(r % 2 * ROUND, (r % 2 + 1) * ROUND)
-            neg_top[r] = gate_tmp.tile([P, ROUND, SOURCES], F32, name="neg_top")
+        def gates_top(k):
+            task_tile, share_tile = logits[k]
+            neg_top[k] = gate_tmp.tile([P, GATE_CHUNK, SOURCES], F32, name="neg_top")
             nc.vector.tensor_reduce(
-                out=neg_top[r][:, :, 0:T], in_=task_tile[:, part], axis=AXIS_X, op=ALU.min
+                out=neg_top[k][:, :, 0:T], in_=task_tile[:], axis=AXIS_X, op=ALU.min
             )
             nc.vector.tensor_reduce(
-                out=neg_top[r][:, :, SHARED], in_=share_tile[:, part], axis=AXIS_X, op=ALU.min
+                out=neg_top[k][:, :, SHARED], in_=share_tile[:], axis=AXIS_X, op=ALU.min
             )
 
         def gates_exp(r, i):
@@ -180,7 +178,7 @@ def tile_plelayer_pa_t_kernel(
                     out=out,
                     in_=in_,
                     func=ACT.Exp,
-                    bias=neg_top[r][:, i, o : o + 1],
+                    bias=neg_top[r // 2][:, at, o : o + 1],
                     scale=-1.0,
                     accum_out=gate_sums[:, n, o, part : part + 1],
                 )
@@ -366,13 +364,24 @@ def tile_plelayer_pa_t_kernel(
                 op=ALU.mult,
             )
 
-        def shared_reduce(r):
-            nc.vector.tensor_reduce(
-                out=shared_sums[r % 2][:, :, 0 : SOURCES * U],
-                in_=shared_prod[r][:].rearrange("b i o u e -> b i (o u) e"),
-                axis=AXIS_X,
+        def shared_halves(r):
+            products = shared_prod[r][:, ROUND - 1].rearrange("b o u e -> b (o u) e")
+            nc.gpsimd.tensor_tensor(
+                out=products[:, :, 0 : E // 2],
+                in0=products[:, :, 0 : E // 2],
+                in1=products[:, :, E // 2 : E],
                 op=ALU.add,
             )
+
+        def shared_reduce(r):
+            products = shared_prod[r][:].rearrange("b i o u e -> b i (o u) e")
+            for rows, experts_left in ((slice(0, ROUND - 1), E), (slice(ROUND - 1, ROUND), E // 2)):
+                nc.vector.tensor_reduce(
+                    out=shared_sums[r % 2][:, rows, 0 : SOURCES * U],
+                    in_=products[:, rows, :, 0:experts_left],
+                    axis=AXIS_X,
+                    op=ALU.add,
+                )
 
         def own_rows(r, i):
             own_ps = ps_own.tile([P, E, T, U], F32, tag="own_ps")
@@ -488,7 +497,9 @@ def tile_plelayer_pa_t_kernel(
             gates_exp(0, i)
         nc.vector.tensor_copy(out=bias_cols[:], in_=bias_ps[:])
         quantize_x(0)
+        regroup_weights(2, nc.scalar.copy)
         expert_group(0, SHARED)
+        regroup_weights(3, nc.scalar.copy)
         regroup_weights(0)
         quantize_weights(0)
         expert_group(0, 0)
@@ -498,20 +509,18 @@ def tile_plelayer_pa_t_kernel(
         transpose_x(1, 0)
         transpose_x(1, 1)
         expert_group(0, 1)
-        regroup_weights(2)
         quantize_weights(2)
         expert_group(0, 2)
-        regroup_weights(3)
         quantize_weights(3)
         transpose_x(1, 2, copy=nc.vector.tensor_copy)
         transpose_x(1, 3, copy=nc.vector.tensor_copy)
         expert_group(0, 3)
-        gates_top(1)
         gates_logits(1)
         quantize_x(1)
         shared_rest(0)
-        gates_top(2)
         shared_products(0)
+        shared_halves(0)
+        gates_top(1)
         transpose_x(2, 0)
         transpose_x(2, 1)
         for i in range(ROUND):
@@ -523,6 +532,8 @@ def tile_plelayer_pa_t_kernel(
         order_x(3, 0)
 
         for s in range(ROUNDS + 3):
+            if s % 2 == 0 and s + 4 < ROUNDS:
+                gates_logits((s + 4) // 2)
             step(expert_group, s + 1, SHARED)
             step(expert_group, s + 1, 0)
             step(order_x, s + 3, 1)
@@ -530,6 +541,8 @@ def tile_plelayer_pa_t_kernel(
             step(own_rows, s, 0)
             step(own_rows, s, 1)
             step(finish, s - 3)
+            if s == ROUNDS - 1:
+                shared_reduce(s)
             step(own_products, s, 0)
             step(sum_over_experts, s - 1, 0)
             step(own_products, s, 1)
@@ -537,6 +550,7 @@ def tile_plelayer_pa_t_kernel(
             step(shared_rows, s + 1)
             step(shared_rest, s + 1)
             step(shared_products, s + 1)
+            step(shared_halves, s + 1)
             step(gates_exp, s + 2, 1)
             step(own_rows, s, 2)
             step(own_products, s, 2)
@@ -554,16 +568,16 @@ def tile_plelayer_pa_t_kernel(
             step(gates_exp, s + 2, 3)
             step(sum_over_experts, s - 1, 2)
             step(expert_group, s + 1, 3)
-            step(shared_reduce, s)
+            if s < ROUNDS - 1:
+                step(shared_reduce, s)
             step(transpose_x, s + 3, 2)
             step(order_x, s + 4, 0)
             step(sum_over_experts, s - 1, 3)
             step(sums_out, s - 1)
             step(transpose_x, s + 3, 3)
             step(transpose_back, s - 2)
-            step(gates_top, s + 3)
-            if s % 2 == 0:
-                step(gates_inverse, s, 2)
-                if s + 4 < ROUNDS:
-                    gates_logits((s + 4) // 2)
+            if s % 2 == 1 and s + 3 < ROUNDS:
+                gates_top((s + 3) // 2)
+            if s % 4 == 2:
+                step(gates_inverse, s - 2, 4)
             step(load_x, s + 3 + X_AHEAD)

@@ -17,6 +17,7 @@ T, B, D, U, E = 4, 8192, 1024, 16, 8
 SOURCES = T + 1
 SHARED = T
 UE = U * E
+PAIRS = E // 2
 G_TASK = 2 * E
 G_SHARE = SOURCES * E
 PACK = 4
@@ -75,7 +76,10 @@ def tile_plelayer_pa_t_kernel(
         load_gates(nc.scalar, 0, 2)
         SHARED_ROW = 32
         bias_rows = keep.tile([P, UE], BF16)
-        nc.scalar.dma_start(out=bias_rows[0:T, :], in_=eb0.rearrange("t u e -> t (u e)"))
+        nc.scalar.dma_start(
+            out=bias_rows[0:PAIRS, :].rearrange("m (c k) -> m c k", k=2),
+            in_=eb0.rearrange("t u (m k) -> m (t u) k", k=2),
+        )
         nc.scalar.dma_start(
             out=bias_rows[SHARED_ROW : SHARED_ROW + 1, :],
             in_=ebs0.rearrange("(o u) e -> o (u e)", o=1),
@@ -220,12 +224,12 @@ def tile_plelayer_pa_t_kernel(
         nc.vector.memset(bias_square[:], 0.0)
 
         bias_cols = keep.tile([P, P], F32)
-        bias_col_of = [t for t in range(T)] + [SHARED_ROW]
+        bias_col_of = [m for m in range(PAIRS)] + [SHARED_ROW]
 
         def expert_biases():
             nc.vector.tensor_copy(
-                out=bias_square[0:T, :].rearrange("t (e u) -> t e u", e=E),
-                in_=bias_rows[0:T, :].rearrange("t (u e) -> t e u", e=E),
+                out=bias_square[0:PAIRS, :].rearrange("m (k c) -> m k c", k=2),
+                in_=bias_rows[0:PAIRS, :].rearrange("m (c k) -> m k c", k=2),
             )
             nc.vector.tensor_copy(
                 out=bias_square[SHARED_ROW : SHARED_ROW + 1, :],
@@ -235,28 +239,38 @@ def tile_plelayer_pa_t_kernel(
             nc.tensor.transpose(out=bias_ps[:], in_=bias_square[:], identity=ident[:])
             return bias_ps
 
-        w_grouped = keep.tile([P, SOURCES, PASSES, UE, PACK], BF16, align_bytes=64)
-        w_codes = keep.tile([P, SOURCES, PASSES, UE], U32, align_bytes=64)
-        w_scales = keep.tile([P, SOURCES, PASSES, UE], U8, align_bytes=64)
+        task_grouped = keep.tile([P, PASSES, E, T, U, PACK], BF16, align_bytes=64)
+        task_codes = keep.tile([P, PASSES, PAIRS * UE], U32, align_bytes=64)
+        task_scales = keep.tile([P, PASSES, PAIRS * UE], U8, align_bytes=64)
+        shared_grouped = keep.tile([P, PASSES, UE, PACK], BF16, align_bytes=64)
+        shared_codes = keep.tile([P, PASSES, UE], U32, align_bytes=64)
+        shared_scales = keep.tile([P, PASSES, UE], U8, align_bytes=64)
 
-        def regroup_weights(group, copy=nc.vector.tensor_copy):
+        def regroup_weights(source, copy=nc.vector.tensor_copy):
             for g in range(PASSES):
-                if group == SHARED:
+                if source == SHARED:
                     copy(
-                        out=w_grouped[:, SHARED, g],
+                        out=shared_grouped[:, g],
                         in_=w_raw[:, SHARED, g].rearrange("q j k -> q k j"),
                     )
                 else:
                     copy(
-                        out=w_grouped[:, group, g].rearrange("q (e u) j -> q e u j", e=E),
-                        in_=w_raw[:, group, g].rearrange("q j (u e) -> q e u j", u=U),
+                        out=task_grouped[:, g, :, source],
+                        in_=w_raw[:, source, g].rearrange("q j (u e) -> q e u j", u=U),
                     )
 
-        def quantize_weights(group):
+        def quantize_shared_weights():
             nc.vector.quantize_mx(
-                out=w_codes[:, group].rearrange("q g k -> q (g k)").bitcast(FP8X4),
-                scales=w_scales[:, group].rearrange("q g k -> q (g k)"),
-                in_=w_grouped[:, group].rearrange("q g k j -> q (g k j)"),
+                out=shared_codes[:].rearrange("q g k -> q (g k)").bitcast(FP8X4),
+                scales=shared_scales[:].rearrange("q g k -> q (g k)"),
+                in_=shared_grouped[:].rearrange("q g k j -> q (g k j)"),
+            )
+
+        def quantize_task_weights(g):
+            nc.vector.quantize_mx(
+                out=task_codes[:, g].bitcast(FP8X4),
+                scales=task_scales[:, g],
+                in_=task_grouped[:, g].rearrange("q e t u j -> q (e t u j)"),
             )
 
         x_words, x_grouped, x_codes, x_scales = {}, {}, {}, {}
@@ -312,12 +326,15 @@ def tile_plelayer_pa_t_kernel(
         def expert_group(r, group):
             if group == SHARED:
                 experts[r] = work.tile([P, SOURCES, COLS], F32, name="experts")
+            columns = slice(0, UE) if group == SHARED else slice(group * UE, (group + 1) * UE)
+            codes = shared_codes if group == SHARED else task_codes
+            scales = shared_scales if group == SHARED else task_scales
             y_ps = ps_y.tile([P, COLS], F32, tag="y_ps")
             for g in range(PASSES):
                 nc.tensor.matmul_mx(
                     out=y_ps[:],
-                    lhsT=w_codes[:, group, g].bitcast(FP8X4),
-                    lhsT_scale=w_scales[:, group, g],
+                    lhsT=codes[:, g, columns].bitcast(FP8X4),
+                    lhsT_scale=scales[:, g, columns],
                     rhs=x_codes[r][:, g, :].bitcast(FP8X4),
                     rhs_scale=x_scales[r][:, g, :],
                     start=(g == 0),
@@ -386,10 +403,10 @@ def tile_plelayer_pa_t_kernel(
         def own_rows(r, i):
             own_ps = ps_own.tile([P, E, T, U], F32, tag="own_ps")
             own_rows_ps[(r, i)] = own_ps
-            for t in range(T):
+            for m in range(PAIRS):
                 nc.tensor.transpose(
-                    out=own_ps[:, :, t, :],
-                    in_=experts[r][:, t, i * P : (i + 1) * P],
+                    out=own_ps[:, 2 * m : 2 * m + 2].rearrange("b e t u -> b (e t u)"),
+                    in_=experts[r][:, m, i * P : (i + 1) * P],
                     identity=ident[:],
                 )
 
@@ -490,34 +507,29 @@ def tile_plelayer_pa_t_kernel(
         for i in range(ROUND):
             transpose_x(0, i)
         regroup_weights(SHARED)
-        quantize_weights(SHARED)
+        quantize_shared_weights()
         bias_ps = expert_biases()
         gates_top(0)
         for i in range(ROUND):
             gates_exp(0, i)
         nc.vector.tensor_copy(out=bias_cols[:], in_=bias_ps[:])
         quantize_x(0)
-        regroup_weights(2, nc.scalar.copy)
-        expert_group(0, SHARED)
         regroup_weights(3, nc.scalar.copy)
-        regroup_weights(0)
-        quantize_weights(0)
-        expert_group(0, 0)
-        regroup_weights(1)
-        quantize_weights(1)
-        shared_rows(0)
+        expert_group(0, SHARED)
+        for t in range(3):
+            regroup_weights(t)
+        for g in range(PASSES):
+            quantize_task_weights(g)
         transpose_x(1, 0)
+        shared_rows(0)
         transpose_x(1, 1)
-        expert_group(0, 1)
-        quantize_weights(2)
-        expert_group(0, 2)
-        quantize_weights(3)
         transpose_x(1, 2, copy=nc.vector.tensor_copy)
         transpose_x(1, 3, copy=nc.vector.tensor_copy)
-        expert_group(0, 3)
-        gates_logits(1)
+        for m in range(PAIRS):
+            expert_group(0, m)
         quantize_x(1)
         shared_rest(0)
+        gates_logits(1)
         shared_products(0)
         shared_halves(0)
         gates_top(1)

@@ -144,20 +144,25 @@ def tile_plelayer_pa_t_kernel(
             )
             nc.vector.tensor_scalar_mul(out=neg_bias[:], in0=spread_ps[:], scalar1=-1.0)
 
-        def gates_logits(k):
-            task_tile = gate_tmp.tile([P, GATE_CHUNK, T, G_TASK], F32)
-            share_tile = gate_tmp.tile([P, GATE_CHUNK, G_SHARE], F32)
-            logits[k] = (task_tile, share_tile)
-            rows = slice(k * GATE_CHUNK, (k + 1) * GATE_CHUNK)
+        def gates_logits(r, count=1):
+            k = r // 2
+            if r % 2 == 0:
+                task_tile = gate_tmp.tile([P, GATE_CHUNK, T, G_TASK], F32)
+                share_tile = gate_tmp.tile([P, GATE_CHUNK, G_SHARE], F32)
+                logits[k] = (task_tile, share_tile)
+            task_tile, share_tile = logits[k]
+            size = count * ROUND
+            rows = slice(r * ROUND, r * ROUND + size)
+            part = slice(r % 2 * ROUND, r % 2 * ROUND + size)
             nc.gpsimd.tensor_tensor(
-                out=task_tile[:],
-                in0=neg_bias_task.unsqueeze(1).to_broadcast([P, GATE_CHUNK, T, G_TASK]),
+                out=task_tile[:, part],
+                in0=neg_bias_task.unsqueeze(1).to_broadcast([P, size, T, G_TASK]),
                 in1=pre_task[:, :, rows, :].rearrange("p t n k -> p n t k"),
                 op=ALU.subtract,
             )
             nc.gpsimd.tensor_tensor(
-                out=share_tile[:],
-                in0=neg_bias_share.unsqueeze(1).to_broadcast([P, GATE_CHUNK, G_SHARE]),
+                out=share_tile[:, part],
+                in0=neg_bias_share.unsqueeze(1).to_broadcast([P, size, G_SHARE]),
                 in1=pre_share[:, rows, :],
                 op=ALU.subtract,
             )
@@ -381,8 +386,11 @@ def tile_plelayer_pa_t_kernel(
                 op=ALU.mult,
             )
 
+        def halved_from(r):
+            return 0 if r == ROUNDS - 1 else ROUND - 1
+
         def shared_halves(r):
-            products = shared_prod[r][:, ROUND - 1].rearrange("b o u e -> b (o u) e")
+            products = shared_prod[r][:, halved_from(r) :].rearrange("b i o u e -> b (i o u) e")
             nc.gpsimd.tensor_tensor(
                 out=products[:, :, 0 : E // 2],
                 in0=products[:, :, 0 : E // 2],
@@ -392,13 +400,15 @@ def tile_plelayer_pa_t_kernel(
 
         def shared_reduce(r):
             products = shared_prod[r][:].rearrange("b i o u e -> b i (o u) e")
-            for rows, experts_left in ((slice(0, ROUND - 1), E), (slice(ROUND - 1, ROUND), E // 2)):
-                nc.vector.tensor_reduce(
-                    out=shared_sums[r % 2][:, rows, 0 : SOURCES * U],
-                    in_=products[:, rows, :, 0:experts_left],
-                    axis=AXIS_X,
-                    op=ALU.add,
-                )
+            cut = halved_from(r)
+            for rows, left in ((slice(0, cut), E), (slice(cut, ROUND), E // 2)):
+                if rows.start < rows.stop:
+                    nc.vector.tensor_reduce(
+                        out=shared_sums[r % 2][:, rows, 0 : SOURCES * U],
+                        in_=products[:, rows, :, 0:left],
+                        axis=AXIS_X,
+                        op=ALU.add,
+                    )
 
         def own_rows(r, i):
             own_ps = ps_own.tile([P, E, T, U], F32, tag="own_ps")
@@ -503,7 +513,7 @@ def tile_plelayer_pa_t_kernel(
                 make(r, *which)
 
         gate_biases()
-        gates_logits(0)
+        gates_logits(0, 2)
         for i in range(ROUND):
             transpose_x(0, i)
         regroup_weights(SHARED)
@@ -527,14 +537,16 @@ def tile_plelayer_pa_t_kernel(
         transpose_x(1, 3, copy=nc.vector.tensor_copy)
         for m in range(PAIRS):
             expert_group(0, m)
+        own_rows(0, 0)
+        own_rows(0, 1)
         quantize_x(1)
         shared_rest(0)
-        gates_logits(1)
+        gates_logits(2, 2)
         shared_products(0)
         shared_halves(0)
         gates_top(1)
-        transpose_x(2, 0)
-        transpose_x(2, 1)
+        transpose_x(2, 0, copy=nc.vector.tensor_copy)
+        transpose_x(2, 1, copy=nc.vector.tensor_copy)
         for i in range(ROUND):
             gates_exp(1, i)
         transpose_x(2, 2)
@@ -544,20 +556,20 @@ def tile_plelayer_pa_t_kernel(
         order_x(3, 0)
 
         for s in range(ROUNDS + 3):
-            if s % 2 == 0 and s + 4 < ROUNDS:
-                gates_logits((s + 4) // 2)
+            step(gates_logits, s + 4)
             step(expert_group, s + 1, SHARED)
             step(expert_group, s + 1, 0)
             step(order_x, s + 3, 1)
             step(gates_exp, s + 2, 0)
-            step(own_rows, s, 0)
-            step(own_rows, s, 1)
+            if s > 0:
+                step(own_rows, s, 0)
+                step(own_rows, s, 1)
             step(finish, s - 3)
-            if s == ROUNDS - 1:
-                shared_reduce(s)
             step(own_products, s, 0)
             step(sum_over_experts, s - 1, 0)
             step(own_products, s, 1)
+            if s == ROUNDS - 1:
+                shared_reduce(s)
             step(quantize_x, s + 2)
             step(shared_rows, s + 1)
             step(shared_rest, s + 1)

from contextlib import ExitStack

import concourse.mybir as mybir
from concourse.masks import make_identity

F32 = mybir.dt.float32
BF16 = mybir.dt.bfloat16
U32 = mybir.dt.uint32
U8 = mybir.dt.uint8
FP8X4 = mybir.dt.float8_e4m3fn_x4
ALU = mybir.AluOpType
ACT = mybir.ActivationFunctionType
AXIS_X = mybir.AxisListType.X

P = 128
T, B, D, U, E = 4, 8192, 1024, 16, 8
SOURCES = T + 1
SHARED = T
UE = U * E
PAIRS = E // 2
G_TASK = 2 * E
G_SHARE = SOURCES * E
PACK = 4
K_PASS = P * PACK
PASSES = D // K_PASS
ROW_TILES = B // P
ROUND = 4
ROUNDS = ROW_TILES // ROUND
COLS = ROUND * P
GATE_CHUNK = 8
STORE_ROUNDS = 2

FLOPS = 2 * B * D * SOURCES * UE


def tile_plelayer_pa_t_kernel(
    tc, x, ews0, ebs0, ew0, eb0, gate_pre0, gb0, sgate_pre, gbs, out_0, out_1
):
    nc = tc.nc
    with ExitStack() as ctx:
        keep = ctx.enter_context(tc.tile_pool(name="keep", bufs=1))
        gate_tmp = ctx.enter_context(tc.tile_pool(name="gate_tmp", bufs=2))
        x_pool = ctx.enter_context(tc.tile_pool(name="x_pool", bufs=3))
        work = ctx.enter_context(tc.tile_pool(name="work", bufs=2))
        words = ctx.enter_context(tc.tile_pool(name="words", bufs=3))
        prod = ctx.enter_context(tc.tile_pool(name="prod", bufs=2 * ROUND))
        ps_y = ctx.enter_context(tc.psum_pool(name="ps_y", bufs=2))
        ps_own = ctx.enter_context(tc.psum_pool(name="ps_own", bufs=4))
        ps_sums = ctx.enter_context(tc.psum_pool(name="ps_sums", bufs=1))
        ps_misc = ctx.enter_context(tc.psum_pool(name="ps_misc", bufs=1))
        ctx.enter_context(tc.manual_schedule())

        x_rows = x.rearrange("(p n) k -> p n k", n=ROW_TILES)
        out_task_rows = out_0.rearrange("t (p n) u -> p t n u", n=ROW_TILES)
        out_share_rows = out_1.rearrange("(p n) u -> p n u", n=ROW_TILES)

        bias_row = keep.tile([P, T * G_TASK + G_SHARE], BF16)
        nc.vector.memset(bias_row[:], 0.0)
        nc.scalar.dma_start(
            out=bias_row[0:1, 0 : T * G_TASK],
            in_=gb0.rearrange("t k -> (t k)").rearrange("(o c) -> o c", o=1),
        )
        nc.scalar.dma_start(
            out=bias_row[0:1, T * G_TASK :], in_=gbs.rearrange("(o c) -> o c", o=1)
        )
        pre_task = keep.tile([P, T, ROW_TILES, G_TASK], BF16)
        pre_share = keep.tile([P, ROW_TILES, G_SHARE], BF16)
        pre_task_rows = gate_pre0.rearrange("t (p n) k -> p t n k", n=ROW_TILES)
        pre_share_rows = sgate_pre.rearrange("(p n) k -> p n k", n=ROW_TILES)

        def load_gates(queue, first, count):
            rows = slice(first * ROUND, (first + count) * ROUND)
            queue.dma_start(out=pre_task[:, :, rows, :], in_=pre_task_rows[:, :, rows, :])
            queue.dma_start(out=pre_share[:, rows, :], in_=pre_share_rows[:, rows, :])

        load_gates(nc.scalar, 0, 2)
        SHARED_ROW = 32
        bias_rows = keep.tile([P, UE], BF16)
        nc.scalar.dma_start(
            out=bias_rows[0:PAIRS, :].rearrange("m (c k) -> m c k", k=2),
            in_=eb0.rearrange("t u (m k) -> m (t u) k", k=2),
        )
        nc.scalar.dma_start(
            out=bias_rows[SHARED_ROW : SHARED_ROW + 1, :],
            in_=ebs0.rearrange("(o u) e -> o (u e)", o=1),
        )

        x_tiles = {}

        def load_x(r, pieces=1):
            x_sb = x_pool.tile([P, ROUND, D], BF16)
            size = ROUND // pieces
            for first in range(0, ROUND, size):
                nc.sync.dma_start(
                    out=x_sb[:, first : first + size, :],
                    in_=x_rows[:, r * ROUND + first : r * ROUND + first + size, :],
                )
            x_tiles[r] = x_sb

        X_AHEAD = 3
        load_x(0, ROUND)
        w_raw = keep.tile([P, SOURCES, PASSES, PACK, UE], BF16)
        nc.sync.dma_start(
            out=w_raw[:, SHARED],
            in_=ews0.rearrange("(g q j) u e -> q g j (u e)", g=PASSES, j=PACK),
        )
        for t in range(T):
            nc.sync.dma_start(
                out=w_raw[:, t],
                in_=ew0[t].rearrange("(g q j) u e -> q g j (u e)", g=PASSES, j=PACK),
            )
        load_x(1, 2)
        load_x(2)
        load_gates(nc.sync, 2, ROUNDS - 2)

        ident = keep.tile([P, P], F32)
        make_identity(nc, ident[:])

        RUN = E
        OWN_STEP, OTHER_STEP = 2 * RUN, 4 * RUN
        GATE_ROW = SOURCES * OTHER_STEP
        gates = keep.tile([P, ROW_TILES * GATE_ROW + 2 * OTHER_STEP], F32)
        gate_inv = keep.tile([P, ROW_TILES, SOURCES], F32)

        def own_gates(n):
            row = gates[:, n * GATE_ROW : n * GATE_ROW + 2 * T * OWN_STEP]
            return row.rearrange("p (j c) -> p j c", c=OWN_STEP)[:, :, RUN:]

        def other_gates(n, count):
            first = n * GATE_ROW + OTHER_STEP
            rows = gates[:, first : first + count * GATE_ROW]
            return rows.rearrange("p (o c) -> p o c", c=OTHER_STEP)[:, :, 0:RUN]

        ones = keep.tile([P, P], BF16)
        nc.vector.memset(ones[:], 1.0)
        neg_bias = keep.tile([P, T * G_TASK + G_SHARE], BF16)
        neg_bias_task = neg_bias[:, 0 : T * G_TASK].rearrange("p (t k) -> p t k", t=T)
        neg_bias_share = neg_bias[:, T * G_TASK :]

        def gate_biases():
            spread_ps = ps_misc.tile([P, T * G_TASK + G_SHARE], F32, tag="misc")
            nc.tensor.matmul(
                out=spread_ps[:], lhsT=ones[:], rhs=bias_row[:], start=True, stop=True
            )
            nc.vector.tensor_scalar_mul(out=neg_bias[:], in0=spread_ps[:], scalar1=-1.0)

        def gates_logits(r, count=1):
            k = r // 2
            if r % 2 == 0:
                task_tile = gate_tmp.tile([P, GATE_CHUNK, T, G_TASK], F32)
                share_tile = gate_tmp.tile([P, GATE_CHUNK, G_SHARE], F32)
                logits[k] = (task_tile, share_tile)
            task_tile, share_tile = logits[k]
            size = count * ROUND
            rows = slice(r * ROUND, r * ROUND + size)
            part = slice(r % 2 * ROUND, r % 2 * ROUND + size)
            nc.gpsimd.tensor_tensor(
                out=task_tile[:, part],
                in0=neg_bias_task.unsqueeze(1).to_broadcast([P, size, T, G_TASK]),
                in1=pre_task[:, :, rows, :].rearrange("p t n k -> p n t k"),
                op=ALU.subtract,
            )
            nc.gpsimd.tensor_tensor(
                out=share_tile[:, part],
                in0=neg_bias_share.unsqueeze(1).to_broadcast([P, size, G_SHARE]),
                in1=pre_share[:, rows, :],
                op=ALU.subtract,
            )

        def gates_top(k):
            task_tile, share_tile = logits[k]
            neg_top[k] = gate_tmp.tile([P, GATE_CHUNK, SOURCES], F32, name="neg_top")
            nc.vector.tensor_reduce(
                out=neg_top[k][:, :, 0:T], in_=task_tile[:], axis=AXIS_X, op=ALU.min
            )
            nc.vector.tensor_reduce(
                out=neg_top[k][:, :, SHARED], in_=share_tile[:], axis=AXIS_X, op=ALU.min
            )

        def gates_exp(r, i):
            task_tile, share_tile = logits[r // 2]
            at = r % 2 * ROUND + i
            n = r * ROUND + i

            def exponentials(out, in_, o, part):
                nc.scalar.activation(
                    out=out,
                    in_=in_,
                    func=ACT.Exp,
                    bias=neg_top[r // 2][:, at, o : o + 1],
                    scale=-1.0,
                    accum_out=gate_sums[:, n, o, part : part + 1],
                )

            for t in range(T):
                own = n * GATE_ROW + t * OWN_STEP + RUN
                step = n * GATE_ROW + (t + 1) * OTHER_STEP - own
                runs = gates[:, own : own + 2 * step].rearrange("p (k c) -> p k c", k=2)
                exponentials(
                    runs[:, :, 0:RUN], task_tile[:, at, t, :].rearrange("p (k e) -> p k e", k=2), t, 0
                )
            exponentials(
                own_gates(n)[:, T:, :],
                share_tile[:, at, 0 : T * E].rearrange("p (t e) -> p t e", t=T),
                SHARED,
                0,
            )
            exponentials(
                other_gates(n, 1)[:, SHARED, :], share_tile[:, at, T * E : G_SHARE], SHARED, 1
            )

        def gates_inverse(r, count):
            rows = slice(r * ROUND, (r + count) * ROUND)
            nc.vector.tensor_reduce(
                out=gate_inv[:, rows, :], in_=gate_sums[:, rows], axis=AXIS_X, op=ALU.add
            )
            nc.vector.reciprocal(out=gate_inv[:, rows, :], in_=gate_inv[:, rows, :])

        logits, neg_top = {}, {}
        gate_sums = keep.tile([P, ROW_TILES, SOURCES, 2], F32)
        nc.vector.memset(gate_sums[:], 0.0)

        shared_sum_a = keep.tile([P, ROUND, P], F32)
        shared_sum_b = keep.tile([P, ROUND, P], F32)
        shared_sums = [shared_sum_a, shared_sum_b]
        for shared_sum in shared_sums:
            nc.gpsimd.memset(shared_sum[:], 0.0)
        bias_square = keep.tile([P, P], F32)
        nc.vector.memset(bias_square[:], 0.0)

        bias_cols = keep.tile([P, P], F32)
        bias_col_of = [m for m in range(PAIRS)] + [SHARED_ROW]

        def expert_biases():
            nc.vector.tensor_copy(
                out=bias_square[0:PAIRS, :].rearrange("m (k c) -> m k c", k=2),
                in_=bias_rows[0:PAIRS, :].rearrange("m (c k) -> m k c", k=2),
            )
            nc.vector.tensor_copy(
                out=bias_square[SHARED_ROW : SHARED_ROW + 1, :],
                in_=bias_rows[SHARED_ROW : SHARED_ROW + 1, :],
            )
            bias_ps = ps_misc.tile([P, P], F32, tag="misc")
            nc.tensor.transpose(out=bias_ps[:], in_=bias_square[:], identity=ident[:])
            return bias_ps

        task_grouped = keep.tile([P, PASSES, E, T, U, PACK], BF16, align_bytes=64)
        task_codes = keep.tile([P, PASSES, PAIRS * UE], U32, align_bytes=64)
        task_scales = keep.tile([P, PASSES, PAIRS * UE], U8, align_bytes=64)
        shared_grouped = keep.tile([P, PASSES, UE, PACK], BF16, align_bytes=64)
        shared_codes = keep.tile([P, PASSES, UE], U32, align_bytes=64)
        shared_scales = keep.tile([P, PASSES, UE], U8, align_bytes=64)

        def regroup_weights(source, copy=nc.vector.tensor_copy):
            for g in range(PASSES):
                if source == SHARED:
                    copy(
                        out=shared_grouped[:, g],
                        in_=w_raw[:, SHARED, g].rearrange("q j k -> q k j"),
                    )
                else:
                    copy(
                        out=task_grouped[:, g, :, source],
                        in_=w_raw[:, source, g].rearrange("q j (u e) -> q e u j", u=U),
                    )

        def quantize_shared_weights():
            nc.vector.quantize_mx(
                out=shared_codes[:].rearrange("q g k -> q (g k)").bitcast(FP8X4),
                scales=shared_scales[:].rearrange("q g k -> q (g k)"),
                in_=shared_grouped[:].rearrange("q g k j -> q (g k j)"),
            )

        def quantize_task_weights(g):
            nc.vector.quantize_mx(
                out=task_codes[:, g].bitcast(FP8X4),
                scales=task_scales[:, g],
                in_=task_grouped[:, g].rearrange("q e t u j -> q (e t u j)"),
            )

        x_words, x_grouped, x_codes, x_scales = {}, {}, {}, {}
        experts, shared_prod, own_prod = {}, {}, {}
        sums_ps, sums_sb, back, own_rows_ps = {}, {}, {}, {}
        shared_rows_ps, shared_rows_sb, share_sums = {}, {}, {}
        SCALAR_COLS = UE - E
        stage_task, stage_share = {}, {}

        UNORDERED_ROUNDS = range(4)

        def unordered(r, i):
            return r in UNORDERED_ROUNDS or i == 3

        def order_x(r, i):
            if unordered(r, i):
                return
            x_words[(r, i)] = words.tile([P, PASSES, 2, P], F32, name="x_words")
            nc.scalar.copy(
                out=x_words[(r, i)][:],
                in_=x_tiles[r][:].bitcast(F32)[:, i, :].rearrange(
                    "b (g q h) -> b g h q", g=PASSES, h=2
                ),
            )

        def transpose_x(r, i, pool=ps_own, tag="own_ps", copy=nc.scalar.copy):
            if i == 0:
                x_grouped[r] = work.tile(
                    [P, PASSES, ROUND, P, PACK], BF16, align_bytes=64, name="x_grouped"
                )
            xt_ps = pool.tile([P, PASSES, 2, P], F32, tag=tag)
            for g in range(PASSES):
                for h in range(2):
                    if unordered(r, i):
                        half = x_tiles[r][:].bitcast(F32)[:, i, 2 * P * g + h : 2 * P * (g + 1) : 2]
                    else:
                        half = x_words[(r, i)][:, g, h, :]
                    nc.tensor.transpose(out=xt_ps[:, g, h, :], in_=half, identity=ident[:])
            copy(
                out=x_grouped[r][:].bitcast(F32)[:, :, i, :, :],
                in_=xt_ps[:].rearrange("q g h b -> q g b h"),
            )

        def quantize_x(r):
            x_codes[r] = work.tile([P, PASSES, COLS], U32, align_bytes=64, name="x_codes")
            x_scales[r] = work.tile([P, PASSES, COLS], U8, align_bytes=64, name="x_scales")
            nc.vector.quantize_mx(
                out=x_codes[r][:].rearrange("q g c -> q (g c)").bitcast(FP8X4),
                scales=x_scales[r][:].rearrange("q g c -> q (g c)"),
                in_=x_grouped[r][:].rearrange("q g i b j -> q (g i b j)"),
            )

        def expert_group(r, group):
            if group == SHARED:
                experts[r] = work.tile([P, SOURCES, COLS], F32, name="experts")
            columns = slice(0, UE) if group == SHARED else slice(group * UE, (group + 1) * UE)
            codes = shared_codes if group == SHARED else task_codes
            scales = shared_scales if group == SHARED else task_scales
            y_ps = ps_y.tile([P, COLS], F32, tag="y_ps")
            for g in range(PASSES):
                nc.tensor.matmul_mx(
                    out=y_ps[:],
                    lhsT=codes[:, g, columns].bitcast(FP8X4),
                    lhsT_scale=scales[:, g, columns],
                    rhs=x_codes[r][:, g, :].bitcast(FP8X4),
                    rhs_scale=x_scales[r][:, g, :],
                    start=(g == 0),
                    stop=(g == PASSES - 1),
                )
            nc.scalar.activation(
                out=experts[r][:, group, :],
                in_=y_ps[:],
                func=ACT.Relu,
                bias=bias_cols[:, bias_col_of[group] : bias_col_of[group] + 1],
                scale=1.0,
            )

        def shared_rows(r):
            shared_ps = ps_misc.tile([P, ROUND, UE], F32, tag="misc")
            shared_rows_ps[r] = shared_ps
            for i in range(ROUND):
                nc.tensor.transpose(
                    out=shared_ps[:, i, :],
                    in_=experts[r][:, SHARED, i * P : (i + 1) * P],
                    identity=ident[:],
                )
            shared_rows_sb[r] = work.tile([P, ROUND, UE], F32, name="shared_rows_sb")
            nc.scalar.copy(
                out=shared_rows_sb[r][:, :, 0:SCALAR_COLS], in_=shared_ps[:, :, 0:SCALAR_COLS]
            )

        def shared_rest(r):
            nc.vector.tensor_copy(
                out=shared_rows_sb[r][:, :, SCALAR_COLS:UE],
                in_=shared_rows_ps[r][:, :, SCALAR_COLS:UE],
            )

        def shared_products(r):
            shared_prod[r] = work.tile([P, ROUND, SOURCES, U, E], F32, name="shared_prod")
            full = [P, ROUND, SOURCES, U, E]
            nc.gpsimd.tensor_tensor(
                out=shared_prod[r][:],
                in0=shared_rows_sb[r][:].rearrange("b i (u e) -> b i u e", e=E).unsqueeze(2).to_broadcast(full),
                in1=other_gates(r * ROUND, ROUND)
                .rearrange("p (i o) e -> p i o e", i=ROUND)
                .unsqueeze(3)
                .to_broadcast(full),
                op=ALU.mult,
            )

        def halved_from(r):
            return 0 if r == ROUNDS - 1 else ROUND - 1

        def shared_halves(r):
            products = shared_prod[r][:, halved_from(r) :].rearrange("b i o u e -> b (i o u) e")
            nc.gpsimd.tensor_tensor(
                out=products[:, :, 0 : E // 2],
                in0=products[:, :, 0 : E // 2],
                in1=products[:, :, E // 2 : E],
                op=ALU.add,
            )

        def shared_reduce(r):
            products = shared_prod[r][:].rearrange("b i o u e -> b i (o u) e")
            cut = halved_from(r)
            for rows, left in ((slice(0, cut), E), (slice(cut, ROUND), E // 2)):
                if rows.start < rows.stop:
                    nc.vector.tensor_reduce(
                        out=shared_sums[r % 2][:, rows, 0 : SOURCES * U],
                        in_=products[:, rows, :, 0:left],
                        axis=AXIS_X,
                        op=ALU.add,
                    )

        def own_rows(r, i):
            own_ps = ps_own.tile([P, E, T, U], F32, tag="own_ps")
            own_rows_ps[(r, i)] = own_ps
            for m in range(PAIRS):
                nc.tensor.transpose(
                    out=own_ps[:, 2 * m : 2 * m + 2].rearrange("b e t u -> b (e t u)"),
                    in_=experts[r][:, m, i * P : (i + 1) * P],
                    identity=ident[:],
                )

        def own_products(r, i):
            own_ps = own_rows_ps[(r, i)]
            own_prod[(r, i)] = prod.tile([P, E, 2, T, U], F32, name="own_prod")
            gate_runs = own_gates(r * ROUND + i).rearrange("p (h t) e -> p e h t", h=2)
            full = [P, E, 2, T, U]
            nc.vector.tensor_tensor(
                out=own_prod[(r, i)][:],
                in0=own_ps[:].unsqueeze(2).to_broadcast(full),
                in1=gate_runs.unsqueeze(4).to_broadcast(full),
                op=ALU.mult,
            )

        def sum_over_experts(r, i):
            if i == 0:
                sums_ps[r] = ps_sums.tile([P, ROUND, P], F32, name="sums_ps")
            for e in range(E):
                nc.tensor.matmul(
                    out=sums_ps[r][:, i, :],
                    lhsT=own_prod[(r, i)][:, e].rearrange("b h t u -> b (h t u)"),
                    rhs=ident[:],
                    is_transpose=True,
                    start=(e == 0),
                    stop=False,
                )
            nc.tensor.matmul(
                out=sums_ps[r][:, i, :],
                lhsT=shared_sums[r % 2][:, i, :],
                rhs=ident[:],
                is_transpose=True,
                start=False,
                stop=True,
            )

        def sums_out(r):
            sums_sb[r] = work.tile([P, ROUND, P], F32, name="sums_sb")
            nc.scalar.copy(out=sums_sb[r][:], in_=sums_ps[r][:])

        def transpose_back(r):
            pool, tag = (ps_misc, "misc") if r < ROUNDS - 2 else (ps_own, "own_ps")
            back[r] = pool.tile([P, ROUND, 2, T, U], F32, tag=tag, name="back_ps")
            for i in range(ROUND):
                nc.tensor.transpose(
                    out=back[r][:, i].rearrange("b h t u -> b (h t u)"),
                    in_=sums_sb[r][:, i, :],
                    identity=ident[:],
                )

        def finish(r):
            batch = r // STORE_ROUNDS
            if r % STORE_ROUNDS == 0:
                stage_task[batch] = work.tile(
                    [P, T, STORE_ROUNDS * ROUND, U], F32, name="stage_task"
                )
                stage_share[batch] = work.tile(
                    [P, STORE_ROUNDS * ROUND, U], F32, name="stage_share"
                )
            at = (r % STORE_ROUNDS) * ROUND
            rows = slice(r * ROUND, (r + 1) * ROUND)
            nc.vector.tensor_tensor(
                out=stage_task[batch][:, :, at : at + ROUND, :].rearrange("b t i u -> b i t u"),
                in0=back[r][:, :, 0],
                in1=gate_inv[:, rows, 0:T].unsqueeze(3).to_broadcast([P, ROUND, T, U]),
                op=ALU.mult,
            )
            nc.vector.tensor_reduce(
                out=stage_share[batch][:, at : at + ROUND, :],
                in_=back[r][:, :, 1].rearrange("b i t u -> b i u t"),
                axis=AXIS_X,
                op=ALU.add,
            )

        def finish_share(r):
            batch = r // STORE_ROUNDS
            at = (r % STORE_ROUNDS) * ROUND
            for i in range(ROUND):
                n = r * ROUND + i
                nc.scalar.activation(
                    out=stage_share[batch][:, at + i, :],
                    in_=stage_share[batch][:, at + i, :],
                    func=ACT.Copy,
                    scale=gate_inv[:, n, SHARED : SHARED + 1],
                )
            if r % STORE_ROUNDS == STORE_ROUNDS - 1:
                n0 = batch * STORE_ROUNDS * ROUND
                n1 = n0 + STORE_ROUNDS * ROUND
                nc.sync.dma_start(out=out_task_rows[:, :, n0:n1, :], in_=stage_task[batch][:])
                nc.sync.dma_start(out=out_share_rows[:, n0:n1, :], in_=stage_share[batch][:])

        def step(make, r, *which):
            if 0 <= r < ROUNDS:
                make(r, *which)

        gate_biases()
        gates_logits(0, 2)
        for i in range(ROUND):
            transpose_x(0, i)
        regroup_weights(SHARED)
        quantize_shared_weights()
        bias_ps = expert_biases()
        gates_top(0)
        for i in range(ROUND):
            gates_exp(0, i)
        nc.vector.tensor_copy(out=bias_cols[:], in_=bias_ps[:])
        quantize_x(0)
        regroup_weights(3, nc.scalar.copy)
        expert_group(0, SHARED)
        for t in range(3):
            regroup_weights(t)
        for g in range(PASSES):
            quantize_task_weights(g)
        transpose_x(1, 0)
        shared_rows(0)
        transpose_x(1, 1)
        transpose_x(1, 2, copy=nc.vector.tensor_copy)
        transpose_x(1, 3, copy=nc.vector.tensor_copy)
        for m in range(PAIRS):
            expert_group(0, m)
        own_rows(0, 0)
        own_rows(0, 1)
        quantize_x(1)
        shared_rest(0)
        gates_logits(2, 2)
        shared_products(0)
        shared_halves(0)
        gates_top(1)
        transpose_x(2, 0, copy=nc.vector.tensor_copy)
        transpose_x(2, 1, copy=nc.vector.tensor_copy)
        for i in range(ROUND):
            gates_exp(1, i)
        transpose_x(2, 2)
        transpose_x(2, 3)
        for r in range(X_AHEAD, 2 * X_AHEAD):
            load_x(r)
        order_x(3, 0)

        for s in range(ROUNDS + 3):
            step(gates_logits, s + 4)
            step(expert_group, s + 1, SHARED)
            step(expert_group, s + 1, 0)
            step(order_x, s + 3, 1)
            step(gates_exp, s + 2, 0)
            if s > 0:
                step(own_rows, s, 0)
                step(own_rows, s, 1)
            step(finish, s - 3)
            step(own_products, s, 0)
            step(sum_over_experts, s - 1, 0)
            step(own_products, s, 1)
            if s == ROUNDS - 1:
                shared_reduce(s)
            step(quantize_x, s + 2)
            step(shared_rows, s + 1)
            step(shared_rest, s + 1)
            step(shared_products, s + 1)
            step(shared_halves, s + 1)
            step(gates_exp, s + 2, 1)
            step(own_rows, s, 2)
            step(own_products, s, 2)
            step(transpose_x, s + 3, 0)
            step(order_x, s + 3, 2)
            step(finish_share, s - 3)
            step(expert_group, s + 1, 1)
            step(expert_group, s + 1, 2)
            step(gates_exp, s + 2, 2)
            step(own_rows, s, 3)
            step(own_products, s, 3)
            step(sum_over_experts, s - 1, 1)
            step(transpose_x, s + 3, 1)
            step(order_x, s + 3, 3)
            step(gates_exp, s + 2, 3)
            step(sum_over_experts, s - 1, 2)
            step(expert_group, s + 1, 3)
            if s < ROUNDS - 1:
                step(shared_reduce, s)
            step(transpose_x, s + 3, 2)
            step(order_x, s + 4, 0)
            step(sum_over_experts, s - 1, 3)
            step(sums_out, s - 1)
            step(transpose_x, s + 3, 3)
            step(transpose_back, s - 2)
            if s % 2 == 1 and s + 3 < ROUNDS:
                gates_top((s + 3) // 2)
            if s % 4 == 2:
                step(gates_inverse, s - 2, 4)
            step(load_x, s + 3 + X_AHEAD)
